import numpy as np
import ml_dtypes


def mxq(x, axis, fmt="e4m3"):
    dtype, down = {"e4m3": (ml_dtypes.float8_e4m3fn, 7), "e5m2": (ml_dtypes.float8_e5m2, 14)}[fmt]
    v = np.moveaxis(np.asarray(x, np.float32).astype(ml_dtypes.bfloat16).astype(np.float64), axis, -1)
    blocks = v.reshape(v.shape[:-1] + (-1, 32))
    amax = np.abs(blocks).max(-1, keepdims=True)
    byte = np.maximum(np.where(amax > 0, np.frexp(amax)[1] - 1 + 127, 0) - down, 1)
    scale = np.exp2(byte - 127.0)
    codes = (blocks / scale).astype(np.float32).astype(dtype).astype(np.float64)
    return np.moveaxis((codes * scale).reshape(v.shape), -1, axis)


WIDE = False


def mx_kscale(k):
    if not WIDE:
        return np.ones(k)
    levels = np.array([10, -10, 5, -5, 0])
    a = np.random.permutation(np.resize(levels, k // 512 * 4)).reshape(k // 512, 4)
    idx = np.arange(k)
    return np.exp2(a[idx // 512, idx % 128 // 32])


BF16 = ml_dtypes.bfloat16


def bf(x):
    return np.asarray(x, np.float32).astype(BF16)


def f64(x):
    return np.asarray(x).astype(np.float64)


E2M1 = np.array([0.0, 0.5, 1.0, 1.5, 2.0, 3.0, 4.0, 6.0, -0.0, -0.5, -1.0, -1.5, -2.0, -3.0, -4.0, -6.0])


def pack_weight(w, fmt):
    k, n = w.shape
    w = f64(bf(w)).reshape(k // 32, 32, n)
    amax = np.abs(w).max(1)
    if fmt == "e4m3":
        byte = np.frexp(amax)[1] - 1 + 127 - 7
    else:
        mant, ex = np.frexp(amax / 6.0)
        byte = np.where(mant > 0.5, ex, ex - 1) + 127
    byte = np.clip(np.where(amax > 0, byte, 1), 1, 254)
    scaled = (w * np.exp2(127.0 - byte)[:, None, :]).reshape(k, n).astype(np.float32)
    by_word = np.ascontiguousarray(scaled.reshape(k // 512, 128, 4, n).transpose(0, 1, 3, 2))
    if fmt == "e4m3":
        words = by_word.astype(ml_dtypes.float8_e4m3fn).view(np.uint8)
    else:
        c = by_word.astype(ml_dtypes.float4_e2m1fn).view(np.uint8) & 0xF
        words = c[..., 0::2] | (c[..., 1::2] << 4)
    return np.ascontiguousarray(words), np.ascontiguousarray(byte.astype(np.uint8).reshape(k // 512, 16, n))


def unpack_weight(words, scales, fmt):
    g, p, n, _ = words.shape
    if fmt == "e4m3":
        vals = np.ascontiguousarray(words).view(ml_dtypes.float8_e4m3fn).astype(np.float64)
    else:
        nib = np.empty((g, p, n, 4), np.uint8)
        nib[..., 0::2] = words & 0xF
        nib[..., 1::2] = words >> 4
        vals = E2M1[nib]
    vals = vals * np.repeat(np.exp2(scales.astype(np.float64) - 127.0), 8, axis=1)[..., None]
    return vals.transpose(0, 1, 3, 2).reshape(g * 512, n)


B, L0, W0, R, DIM, OUT = 128, 16, 8, 32, 2048, 512
K1 = L0 * W0
KR = R * R
EPS = 1e-5
FMT = "e4m3"


def setup_inputs():
    s2, s3 = mx_kscale(KR), mx_kscale(KR)
    rn = np.random.standard_normal
    d = {
        "x": bf(rn((B, L0, W0))),
        "km1": bf(rn((L0, W0, DIM)) / np.sqrt(K1)),
        "b1": bf(0.5 + 0.3 * rn(DIM)),
        "t2": bf(rn((B, R, R)) * s2.reshape(R, R)),
        "core2": bf(rn((R, R, DIM)) / np.sqrt(KR) / s2.reshape(R, R, 1)),
        "t3": bf(rn((B, R, R)) * s3.reshape(R, R)),
        "core3": bf(rn((R, R, DIM)) / np.sqrt(KR) / s3.reshape(R, R, 1)),
        "ln_g": bf(1.0 + 0.1 * rn(DIM)),
        "ln_b": bf(0.1 * rn(DIM)),
    }
    fc_w = rn((OUT, DIM)) / np.sqrt(DIM)
    words, scales = pack_weight(np.ascontiguousarray(fc_w.T), FMT)
    d["fc_w_words"] = words
    d["fc_w_scales"] = scales
    d["fc_b"] = bf(0.3 * rn(OUT))
    return d


def reference(x, km1, b1, t2, core2, t3, core3, ln_g, ln_b, fc_w_words, fc_w_scales, fc_b):
    o = f64(x).reshape(B, K1) @ f64(km1).reshape(K1, DIM) + f64(b1)
    o = o + (mxq(f64(t2).reshape(B, KR), 1, "e4m3") @ mxq(f64(core2).reshape(KR, DIM), 0, "e4m3"))
    o = o + (mxq(f64(t3).reshape(B, KR), 1, "e4m3") @ mxq(f64(core3).reshape(KR, DIM), 0, "e4m3"))
    mu = o.mean(-1, keepdims=True)
    var = ((o - mu) ** 2).mean(-1, keepdims=True)
    y = (o - mu) / np.sqrt(var + EPS) * f64(ln_g) + f64(ln_b)
    out = (mxq(y, 1, "e4m3") @ unpack_weight(fc_w_words, fc_w_scales, FMT)) + f64(fc_b)
    return out[:, None, :]

@@ -1,0 +1,250 @@
+from contextlib import ExitStack
+
+import concourse.mybir as mybir
+from concourse.masks import make_identity
+
+F32 = mybir.dt.float32
+BF16 = mybir.dt.bfloat16
+U32 = mybir.dt.uint32
+U8 = mybir.dt.uint8
+I32 = mybir.dt.int32
+FP8X4 = mybir.dt.float8_e4m3fn_x4
+ALU = mybir.AluOpType
+ACT = mybir.ActivationFunctionType
+
+P = 128
+PACK = 4
+K_PASS = P * PACK
+K1 = 128
+KR = 1024
+DIM = 2048
+OUT = 512
+BANK = 512
+N_BANKS = DIM // BANK
+CORE_PASSES = KR // K_PASS
+PASSES = 2 * CORE_PASSES
+CHUNK = 2 * BANK
+RUN = 4
+EPS = 1e-5
+
+FLOPS = 2 * P * (K1 + 2 * KR) * DIM + 2 * P * DIM * OUT
+
+
+def regroup(copy, grouped, rows):
+    copy(
+        out=grouped.rearrange("p (c i) j -> p c j i", i=RUN),
+        in_=rows.rearrange("p j (c i) -> p c j i", i=RUN),
+    )
+
+
+def tile_pinmodel_pa_kernel(
+    tc, x, km1, b1, t2, core2, t3, core3, ln_g, ln_b, fc_w_words, fc_w_scales, fc_b, out
+):
+    nc = tc.nc
+    with ExitStack() as ctx:
+        keep = ctx.enter_context(tc.tile_pool(name="keep", bufs=1))
+        raw_pool = ctx.enter_context(tc.tile_pool(name="raw", bufs=PASSES * DIM // CHUNK))
+        grouped_pool = ctx.enter_context(tc.tile_pool(name="grouped", bufs=4))
+        acc_pool = ctx.enter_context(tc.psum_pool(name="acc", bufs=1))
+        work = ctx.enter_context(tc.psum_pool(name="work", bufs=4))
+
+        b1_rows = keep.tile([P, DIM], BF16)
+        nc.vector.memset(b1_rows[:], 0.0)
+        ones = keep.tile([P, P], BF16)
+        nc.vector.memset(ones[:], 1.0)
+        eps = keep.tile([P, 1], F32)
+        nc.vector.memset(eps[:], EPS)
+        w_planes = keep.tile([P, OUT], U8, align_bytes=64)
+        nc.vector.memset(w_planes[:].bitcast(I32), 0)
+        warm = keep.tile([P, 1], F32)
+        nc.scalar.sqrt(out=warm[:], in_=eps[:])
+        ident_f32 = keep.tile([P, P], F32)
+        make_identity(nc, ident_f32[:])
+        ident_bf16 = keep.tile([P, P], BF16)
+        make_identity(nc, ident_bf16[:])
+
+        x_sb = keep.tile([P, K1], BF16)
+        nc.sync.dma_start(out=x_sb[:], in_=x.rearrange("b i j -> b (i j)"))
+        km1_sb = keep.tile([P, DIM], BF16)
+        nc.sync.dma_start(out=km1_sb[:], in_=km1.rearrange("i j n -> (i j) n"))
+        nc.scalar.dma_start(out=b1_rows[0:1, :], in_=b1.unsqueeze(0))
+        t_sb = []
+        for name, t_dram in (("t2_sb", t2), ("t3_sb", t3)):
+            t_tile = keep.tile([P, KR], BF16, name=name)
+            nc.sync.dma_start(out=t_tile[:], in_=t_dram.rearrange("b p q -> b (p q)"))
+            t_sb.append(t_tile)
+        gain_bias_bf16 = keep.tile([P, 2, N_BANKS * PACK], BF16)
+        with nc.allow_non_contiguous_dma(reason="two vectors of 2048, in pieces of 8 bytes"):
+            for i, vec in enumerate((ln_g, ln_b)):
+                nc.scalar.dma_start(
+                    out=gain_bias_bf16[:, i, :].rearrange("p (g t) -> p g t", t=PACK),
+                    in_=vec.rearrange("(g p t) -> p g t", p=P, t=PACK),
+                )
+        raw = {}
+        for c in range(PASSES):
+            core = (core2, core3)[c // CORE_PASSES].rearrange("p q n -> (p q) n")
+            first = (c % CORE_PASSES) * K_PASS
+            rows = core[first : first + K_PASS, :].rearrange("(p j) n -> p j n", j=PACK)
+            for h in range(DIM // CHUNK):
+                raw_tile = raw_pool.tile([P, PACK, CHUNK], BF16, name="raw_tile")
+                nc.sync.dma_start(out=raw_tile[:], in_=rows[:, :, h * CHUNK : (h + 1) * CHUNK])
+                raw[(c, h)] = raw_tile
+        scale_words = fc_w_scales.bitcast(I32)
+        for quadrant in range(4):
+            nc.sync.dma_start(
+                out=w_planes[:].bitcast(I32)[32 * quadrant : 32 * quadrant + 16, :],
+                in_=scale_words[:, 4 * quadrant : 4 * quadrant + 4, :],
+            )
+        w_words = keep.tile([P, N_BANKS, OUT], U32, align_bytes=64)
+        nc.sync.dma_start(
+            out=w_words[:].bitcast(I32),
+            in_=fc_w_words.rearrange("g p n t -> p g (n t)").bitcast(I32),
+        )
+        fc_b_all = keep.tile([P, OUT], BF16)
+        nc.sync.dma_start(out=fc_b_all[:], in_=fc_b.partition_broadcast(P))
+
+        xT_ps = work.tile([P, P], BF16, tag="work")
+        nc.tensor.transpose(out=xT_ps[:], in_=x_sb[:], identity=ident_bf16[:])
+        xT = keep.tile([P, P], BF16)
+        nc.vector.tensor_copy(out=xT[:], in_=xT_ps[:])
+        o1 = keep.tile([P, N_BANKS, PACK, P], F32)
+        for g in range(N_BANKS):
+            cols = slice(g * BANK, (g + 1) * BANK)
+            o1_ps = work.tile([P, BANK], F32, tag="work")
+            nc.tensor.matmul(out=o1_ps[:], lhsT=xT[:], rhs=km1_sb[:, cols], start=True, stop=False)
+            nc.tensor.matmul(out=o1_ps[:], lhsT=ones[:], rhs=b1_rows[:, cols], start=False, stop=True)
+            copy = nc.vector.tensor_copy if g % 2 == 0 else nc.scalar.copy
+            copy(out=o1[:, g, :, :], in_=o1_ps[:].rearrange("r (p t) -> r t p", t=PACK))
+
+        t_codes = keep.tile([P, PASSES, P], U32, align_bytes=64)
+        t_scales = keep.tile([P, PASSES, P], U8, align_bytes=64)
+        for i in range(2):
+            words = t_sb[i][:].bitcast(F32)
+            tT_ps = work.tile([P, CORE_PASSES, 2, P], F32, tag="work")
+            for g in range(CORE_PASSES):
+                for u in range(2):
+                    nc.tensor.transpose(
+                        out=tT_ps[:, g, u, :],
+                        in_=words[:, g * K_PASS // 2 + u : (g + 1) * K_PASS // 2 : 2],
+                        identity=ident_f32[:],
+                    )
+            t_grouped = keep.tile([P, KR], BF16, name="t_grouped%d" % i, align_bytes=64)
+            copy = nc.vector.tensor_copy if i == 0 else nc.scalar.copy
+            copy(
+                out=t_grouped[:].bitcast(F32).rearrange("p (g r u) -> p g r u", g=CORE_PASSES, u=2),
+                in_=tT_ps[:].rearrange("p g u r -> p g r u"),
+            )
+            passes = slice(i * CORE_PASSES, (i + 1) * CORE_PASSES)
+            nc.vector.quantize_mx(
+                out=t_codes[:, passes, :].rearrange("p g r -> p (g r)").bitcast(FP8X4),
+                scales=t_scales[:, passes, :].rearrange("p g r -> p (g r)"),
+                in_=t_grouped[:],
+            )
+
+        gain_bias = keep.tile([P, 2, N_BANKS * PACK], F32)
+        nc.vector.tensor_copy(out=gain_bias[:], in_=gain_bias_bf16[:])
+
+        c_codes = keep.tile([P, PASSES, DIM], U32, align_bytes=64)
+        c_scales = keep.tile([P, PASSES, DIM], U8, align_bytes=64)
+        acc = [acc_pool.tile([P, BANK], F32, name="acc%d" % g) for g in range(N_BANKS)]
+        for c in range(PASSES):
+            for h in range(DIM // CHUNK):
+                for u, copy in enumerate((nc.vector.tensor_copy, nc.scalar.copy)):
+                    g = h * (CHUNK // BANK) + u
+                    cols = slice(g * BANK, (g + 1) * BANK)
+                    grouped = grouped_pool.tile([P, BANK, PACK], BF16, align_bytes=64)
+                    regroup(copy, grouped[:], raw[(c, h)][:, :, u * BANK : (u + 1) * BANK])
+                    nc.vector.quantize_mx(
+                        out=c_codes[:, c, cols].bitcast(FP8X4),
+                        scales=c_scales[:, c, cols],
+                        in_=grouped[:].rearrange("p w j -> p (w j)"),
+                    )
+                    nc.tensor.matmul_mx(
+                        out=acc[g][:],
+                        lhsT=t_codes[:, c, :].bitcast(FP8X4),
+                        lhsT_scale=t_scales[:, c, :],
+                        rhs=c_codes[:, c, cols].bitcast(FP8X4),
+                        rhs_scale=c_scales[:, c, cols],
+                        start=(c == 0),
+                        stop=(c == PASSES - 1),
+                    )
+
+        o = keep.tile([P, N_BANKS, PACK, P], F32)
+        stats = keep.tile([P, N_BANKS, 6], F32)
+        for g in range(N_BANKS):
+            nc.vector.tensor_tensor(
+                out=o[:, g, :, :],
+                in0=acc[g][:].rearrange("r (p t) -> r t p", t=PACK),
+                in1=o1[:, g, :, :],
+                op=ALU.add,
+            )
+            nc.vector.bn_stats(out=stats[:, g, :], in_=o[:, g, :, :].rearrange("r t p -> r (t p)"))
+        mean_var = keep.tile([P, 2], F32)
+        nc.vector.bn_aggr(out=mean_var[:], in_=stats[:].rearrange("r g s -> r (g s)"))
+        std = keep.tile([P, 1], F32)
+        nc.scalar.activation(out=std[:], in_=mean_var[:, 1:2], func=ACT.Sqrt, bias=eps[:], scale=1.0)
+        rstd = keep.tile([P, 1], F32)
+        nc.vector.reciprocal(out=rstd[:], in_=std[:])
+
+        z = keep.tile([P, N_BANKS, PACK, P], F32)
+        y_planes = keep.tile([P, N_BANKS, PACK, P], BF16)
+        y_grouped = keep.tile([P, N_BANKS, P, PACK], BF16, align_bytes=64)
+        y_codes = keep.tile([P, N_BANKS, P], U32, align_bytes=64)
+        y_scales = keep.tile([P, N_BANKS, P], U8, align_bytes=64)
+        for g in range(N_BANKS):
+            nc.vector.tensor_scalar(
+                out=z[:, g, :, :],
+                in0=o[:, g, :, :],
+                scalar1=mean_var[:, 0:1],
+                scalar2=rstd[:],
+                op0=ALU.subtract,
+                op1=ALU.mult,
+            )
+        for g in range(N_BANKS):
+            for half in range(2):
+                zT_ps = work.tile([P, 2, P], F32, tag="work")
+                for e in range(2):
+                    t = 2 * half + e
+                    nc.tensor.transpose(out=zT_ps[:, e, :], in_=z[:, g, t, :], identity=ident_f32[:])
+                for e in range(2):
+                    t = 2 * half + e
+                    k = g * PACK + t
+                    if half == 0:
+                        nc.scalar.activation(
+                            out=y_planes[:, g, t, :],
+                            in_=zT_ps[:, e, :],
+                            func=ACT.Identity,
+                            bias=gain_bias[:, 1, k : k + 1],
+                            scale=gain_bias[:, 0, k : k + 1],
+                        )
+                    else:
+                        nc.vector.tensor_scalar(
+                            out=y_planes[:, g, t, :],
+                            in0=zT_ps[:, e, :],
+                            scalar1=gain_bias[:, 0, k : k + 1],
+                            scalar2=gain_bias[:, 1, k : k + 1],
+                            op0=ALU.mult,
+                            op1=ALU.add,
+                        )
+        for g in range(N_BANKS):
+            regroup(nc.vector.tensor_copy, y_grouped[:, g, :, :], y_planes[:, g, :, :])
+        for g in range(N_BANKS):
+            nc.vector.quantize_mx(
+                out=y_codes[:, g, :].bitcast(FP8X4),
+                scales=y_scales[:, g, :],
+                in_=y_grouped[:, g, :, :].rearrange("p r t -> p (r t)"),
+            )
+        out_ps = work.tile([P, OUT], F32, tag="work")
+        for g in range(N_BANKS):
+            nc.tensor.matmul_mx(
+                out=out_ps[:],
+                lhsT=y_codes[:, g, :].bitcast(FP8X4),
+                lhsT_scale=y_scales[:, g, :],
+                rhs=w_words[:, g, :].bitcast(FP8X4),
+                rhs_scale=w_planes[PACK * g : P, :],
+                start=(g == 0),
+                stop=(g == N_BANKS - 1),
+            )
+        out_sb = keep.tile([P, OUT], F32)
+        nc.vector.tensor_tensor(out=out_sb[:], in0=out_ps[:], in1=fc_b_all[:], op=ALU.add)
+        nc.sync.dma_start(out=out.rearrange("b o n -> b (o n)"), in_=out_sb[:])

@@ -23,11 +23,14 @@ BANK = 512
 N_BANKS = DIM // BANK
 CORE_PASSES = KR // K_PASS
 PASSES = 2 * CORE_PASSES
-CHUNK = 2 * BANK
 RUN = 4
 EPS = 1e-5
 
 FLOPS = 2 * P * (K1 + 2 * KR) * DIM + 2 * P * DIM * OUT
+
+
+PIECES = ((512, 512, 1024), (1024, 1024), (1024, 1024), (1024, 512, 512))
+VECTOR_COLS = (320, 256, 256, 128)
 
 
 def regroup(copy, grouped, rows):
@@ -43,13 +46,17 @@ def tile_pinmodel_pa_kernel(
     nc = tc.nc
     with ExitStack() as ctx:
         keep = ctx.enter_context(tc.tile_pool(name="keep", bufs=1))
-        raw_pool = ctx.enter_context(tc.tile_pool(name="raw", bufs=PASSES * DIM // CHUNK))
         grouped_pool = ctx.enter_context(tc.tile_pool(name="grouped", bufs=4))
         acc_pool = ctx.enter_context(tc.psum_pool(name="acc", bufs=1))
         work = ctx.enter_context(tc.psum_pool(name="work", bufs=4))
+        ctx.enter_context(tc.manual_schedule())
 
         b1_rows = keep.tile([P, DIM], BF16)
-        nc.vector.memset(b1_rows[:], 0.0)
+        nc.gpsimd.memset(b1_rows[:].bitcast(I32), 0)
+        ident_bf16 = keep.tile([P, P], BF16)
+        make_identity(nc, ident_bf16[:])
+        ident_f32 = keep.tile([P, P], F32)
+        make_identity(nc, ident_f32[:])
         ones = keep.tile([P, P], BF16)
         nc.vector.memset(ones[:], 1.0)
         eps = keep.tile([P, 1], F32)
@@ -58,37 +65,46 @@ def tile_pinmodel_pa_kernel(
         nc.vector.memset(w_planes[:].bitcast(I32), 0)
         warm = keep.tile([P, 1], F32)
         nc.scalar.sqrt(out=warm[:], in_=eps[:])
-        ident_f32 = keep.tile([P, P], F32)
-        make_identity(nc, ident_f32[:])
-        ident_bf16 = keep.tile([P, P], BF16)
-        make_identity(nc, ident_bf16[:])
+
+        cores = [t.rearrange("p q n -> (p q) n") for t in (core2, core3)]
+        raw = {}
+
+        def load_core(c, piece):
+            width = PIECES[c][piece]
+            begin = sum(PIECES[c][:piece])
+            first = (c % CORE_PASSES) * K_PASS
+            rows = cores[c // CORE_PASSES][first : first + K_PASS, :]
+            raw_tile = keep.tile([P, PACK, width], BF16, name="raw%d_%d" % (c, piece))
+            nc.sync.dma_start(
+                out=raw_tile[:],
+                in_=rows.rearrange("(p j) n -> p j n", j=PACK)[:, :, begin : begin + width],
+            )
+            for b in range(width // BANK):
+                raw[(c, begin // BANK + b)] = raw_tile[:, :, b * BANK : (b + 1) * BANK]
 
         x_sb = keep.tile([P, K1], BF16)
-        nc.sync.dma_start(out=x_sb[:], in_=x.rearrange("b i j -> b (i j)"))
+        t_sb = [keep.tile([P, KR], BF16, name="t_sb%d" % i) for i in range(2)]
         km1_sb = keep.tile([P, DIM], BF16)
+        load_core(0, 0)
+        nc.sync.dma_start(out=x_sb[:], in_=x.rearrange("b i j -> b (i j)"))
+        nc.sync.dma_start(out=t_sb[0][:], in_=t2.rearrange("b p q -> b (p q)"))
+        load_core(0, 1)
         nc.sync.dma_start(out=km1_sb[:], in_=km1.rearrange("i j n -> (i j) n"))
-        nc.scalar.dma_start(out=b1_rows[0:1, :], in_=b1.unsqueeze(0))
-        t_sb = []
-        for name, t_dram in (("t2_sb", t2), ("t3_sb", t3)):
-            t_tile = keep.tile([P, KR], BF16, name=name)
-            nc.sync.dma_start(out=t_tile[:], in_=t_dram.rearrange("b p q -> b (p q)"))
-            t_sb.append(t_tile)
+        nc.sync.dma_start(out=b1_rows[0:1, :], in_=b1.unsqueeze(0))
+        load_core(0, 2)
+        load_core(1, 0)
+        nc.sync.dma_start(out=t_sb[1][:], in_=t3.rearrange("b p q -> b (p q)"))
+        load_core(1, 1)
+        for c in (2, 3):
+            for piece in range(len(PIECES[c])):
+                load_core(c, piece)
         gain_bias_bf16 = keep.tile([P, 2, N_BANKS * PACK], BF16)
         with nc.allow_non_contiguous_dma(reason="two vectors of 2048, in pieces of 8 bytes"):
             for i, vec in enumerate((ln_g, ln_b)):
-                nc.scalar.dma_start(
+                nc.sync.dma_start(
                     out=gain_bias_bf16[:, i, :].rearrange("p (g t) -> p g t", t=PACK),
                     in_=vec.rearrange("(g p t) -> p g t", p=P, t=PACK),
                 )
-        raw = {}
-        for c in range(PASSES):
-            core = (core2, core3)[c // CORE_PASSES].rearrange("p q n -> (p q) n")
-            first = (c % CORE_PASSES) * K_PASS
-            rows = core[first : first + K_PASS, :].rearrange("(p j) n -> p j n", j=PACK)
-            for h in range(DIM // CHUNK):
-                raw_tile = raw_pool.tile([P, PACK, CHUNK], BF16, name="raw_tile")
-                nc.sync.dma_start(out=raw_tile[:], in_=rows[:, :, h * CHUNK : (h + 1) * CHUNK])
-                raw[(c, h)] = raw_tile
         scale_words = fc_w_scales.bitcast(I32)
         for quadrant in range(4):
             nc.sync.dma_start(
@@ -103,22 +119,49 @@ def tile_pinmodel_pa_kernel(
         fc_b_all = keep.tile([P, OUT], BF16)
         nc.sync.dma_start(out=fc_b_all[:], in_=fc_b.partition_broadcast(P))
 
-        xT_ps = work.tile([P, P], BF16, tag="work")
-        nc.tensor.transpose(out=xT_ps[:], in_=x_sb[:], identity=ident_bf16[:])
-        xT = keep.tile([P, P], BF16)
-        nc.vector.tensor_copy(out=xT[:], in_=xT_ps[:])
-        o1 = keep.tile([P, N_BANKS, PACK, P], F32)
-        for g in range(N_BANKS):
-            cols = slice(g * BANK, (g + 1) * BANK)
-            o1_ps = work.tile([P, BANK], F32, tag="work")
-            nc.tensor.matmul(out=o1_ps[:], lhsT=xT[:], rhs=km1_sb[:, cols], start=True, stop=False)
-            nc.tensor.matmul(out=o1_ps[:], lhsT=ones[:], rhs=b1_rows[:, cols], start=False, stop=True)
-            copy = nc.vector.tensor_copy if g % 2 == 0 else nc.scalar.copy
-            copy(out=o1[:, g, :, :], in_=o1_ps[:].rearrange("r (p t) -> r t p", t=PACK))
-
+        c_codes = keep.tile([P, PASSES, DIM], U32, align_bytes=64)
+        c_scales = keep.tile([P, PASSES, DIM], U8, align_bytes=64)
         t_codes = keep.tile([P, PASSES, P], U32, align_bytes=64)
         t_scales = keep.tile([P, PASSES, P], U8, align_bytes=64)
-        for i in range(2):
+        acc = [acc_pool.tile([P, BANK], F32, name="acc%d" % g) for g in range(N_BANKS)]
+        o1 = keep.tile([P, N_BANKS, PACK, P], F32)
+        o = keep.tile([P, N_BANKS, PACK, P], F32)
+        stats = keep.tile([P, N_BANKS, 6], F32)
+        xT = keep.tile([P, P], BF16)
+        grouped = {}
+
+        def regroup_bank(c, g):
+            tile = grouped_pool.tile([P, BANK, PACK], BF16, name="grouped_bank", align_bytes=64)
+            split = VECTOR_COLS[c]
+            regroup(nc.vector.tensor_copy, tile[:, :split, :], raw[(c, g)][:, :, :split])
+            regroup(nc.scalar.copy, tile[:, split:, :], raw[(c, g)][:, :, split:])
+            grouped[(c, g)] = tile
+
+        def multiply_bank(c, g):
+            cols = slice(g * BANK, (g + 1) * BANK)
+            nc.vector.quantize_mx(
+                out=c_codes[:, c, cols].bitcast(FP8X4),
+                scales=c_scales[:, c, cols],
+                in_=grouped[(c, g)][:].rearrange("p w j -> p (w j)"),
+            )
+            nc.tensor.matmul_mx(
+                out=acc[g][:],
+                lhsT=t_codes[:, c, :].bitcast(FP8X4),
+                lhsT_scale=t_scales[:, c, :],
+                rhs=c_codes[:, c, cols].bitcast(FP8X4),
+                rhs_scale=c_scales[:, c, cols],
+                start=(c == 0),
+                stop=(c == PASSES - 1),
+            )
+
+        def transpose_x():
+            xT_ps = work.tile([P, P], BF16, tag="work")
+            nc.tensor.transpose(out=xT_ps[:], in_=x_sb[:], identity=ident_bf16[:])
+            nc.scalar.copy(out=xT[:], in_=xT_ps[:])
+
+        t_grouped = {}
+
+        def transpose_t(i):
             words = t_sb[i][:].bitcast(F32)
             tT_ps = work.tile([P, CORE_PASSES, 2, P], F32, tag="work")
             for g in range(CORE_PASSES):
@@ -128,57 +171,76 @@ def tile_pinmodel_pa_kernel(
                         in_=words[:, g * K_PASS // 2 + u : (g + 1) * K_PASS // 2 : 2],
                         identity=ident_f32[:],
                     )
-            t_grouped = keep.tile([P, KR], BF16, name="t_grouped%d" % i, align_bytes=64)
-            copy = nc.vector.tensor_copy if i == 0 else nc.scalar.copy
-            copy(
-                out=t_grouped[:].bitcast(F32).rearrange("p (g r u) -> p g r u", g=CORE_PASSES, u=2),
+            t_grouped[i] = keep.tile([P, KR], BF16, name="t_grouped%d" % i, align_bytes=64)
+            nc.scalar.copy(
+                out=t_grouped[i][:].bitcast(F32).rearrange("p (g r u) -> p g r u", g=CORE_PASSES, u=2),
                 in_=tT_ps[:].rearrange("p g u r -> p g r u"),
             )
+
+        def quantize_t(i):
             passes = slice(i * CORE_PASSES, (i + 1) * CORE_PASSES)
             nc.vector.quantize_mx(
                 out=t_codes[:, passes, :].rearrange("p g r -> p (g r)").bitcast(FP8X4),
                 scales=t_scales[:, passes, :].rearrange("p g r -> p (g r)"),
-                in_=t_grouped[:],
+                in_=t_grouped[i][:],
             )
 
-        gain_bias = keep.tile([P, 2, N_BANKS * PACK], F32)
-        nc.vector.tensor_copy(out=gain_bias[:], in_=gain_bias_bf16[:])
+        o1_ps = {}
 
-        c_codes = keep.tile([P, PASSES, DIM], U32, align_bytes=64)
-        c_scales = keep.tile([P, PASSES, DIM], U8, align_bytes=64)
-        acc = [acc_pool.tile([P, BANK], F32, name="acc%d" % g) for g in range(N_BANKS)]
-        for c in range(PASSES):
-            for h in range(DIM // CHUNK):
-                for u, copy in enumerate((nc.vector.tensor_copy, nc.scalar.copy)):
-                    g = h * (CHUNK // BANK) + u
-                    cols = slice(g * BANK, (g + 1) * BANK)
-                    grouped = grouped_pool.tile([P, BANK, PACK], BF16, align_bytes=64)
-                    regroup(copy, grouped[:], raw[(c, h)][:, :, u * BANK : (u + 1) * BANK])
-                    nc.vector.quantize_mx(
-                        out=c_codes[:, c, cols].bitcast(FP8X4),
-                        scales=c_scales[:, c, cols],
-                        in_=grouped[:].rearrange("p w j -> p (w j)"),
-                    )
-                    nc.tensor.matmul_mx(
-                        out=acc[g][:],
-                        lhsT=t_codes[:, c, :].bitcast(FP8X4),
-                        lhsT_scale=t_scales[:, c, :],
-                        rhs=c_codes[:, c, cols].bitcast(FP8X4),
-                        rhs_scale=c_scales[:, c, cols],
-                        start=(c == 0),
-                        stop=(c == PASSES - 1),
-                    )
+        def order_1(g):
+            cols = slice(g * BANK, (g + 1) * BANK)
+            o1_ps[g] = work.tile([P, BANK], F32, name="o1_ps", tag="work")
+            nc.tensor.matmul(out=o1_ps[g][:], lhsT=xT[:], rhs=km1_sb[:, cols], start=True, stop=False)
+            nc.tensor.matmul(out=o1_ps[g][:], lhsT=ones[:], rhs=b1_rows[:, cols], start=False, stop=True)
 
-        o = keep.tile([P, N_BANKS, PACK, P], F32)
-        stats = keep.tile([P, N_BANKS, 6], F32)
-        for g in range(N_BANKS):
+        def keep_order_1(g):
+            nc.scalar.copy(out=o1[:, g, :, :], in_=o1_ps[g][:].rearrange("r (p t) -> r t p", t=PACK))
+
+        def add_orders(g):
             nc.vector.tensor_tensor(
                 out=o[:, g, :, :],
                 in0=acc[g][:].rearrange("r (p t) -> r t p", t=PACK),
                 in1=o1[:, g, :, :],
                 op=ALU.add,
             )
+
+        def row_stats(g):
             nc.vector.bn_stats(out=stats[:, g, :], in_=o[:, g, :, :].rearrange("r t p -> r (t p)"))
+
+        steps = [(c, g) for c in range(PASSES) for g in range(N_BANKS)]
+        last = len(steps) - 1
+        regroup_bank(*steps[0])
+        for i, (c, g) in enumerate(steps):
+            if i < last:
+                regroup_bank(*steps[i + 1])
+            if i == 0:
+                transpose_x()
+                transpose_t(0)
+                quantize_t(0)
+                order_1(0)
+                order_1(1)
+                keep_order_1(0)
+            if 1 <= i < N_BANKS:
+                keep_order_1(i)
+                if i + 1 < N_BANKS:
+                    order_1(i + 1)
+            if i == 5:
+                transpose_t(1)
+            if i == 6:
+                quantize_t(1)
+            multiply_bank(c, g)
+            if i >= last - 1:
+                add_orders(i - last + 1)
+            if i == last:
+                row_stats(0)
+        add_orders(2)
+        row_stats(1)
+        add_orders(3)
+        row_stats(2)
+        row_stats(3)
+
+        gain_bias = keep.tile([P, 2, N_BANKS * PACK], F32)
+        nc.scalar.copy(out=gain_bias[:], in_=gain_bias_bf16[:])
         mean_var = keep.tile([P, 2], F32)
         nc.vector.bn_aggr(out=mean_var[:], in_=stats[:].rearrange("r g s -> r (g s)"))
         std = keep.tile([P, 1], F32)
@@ -200,42 +262,27 @@ def tile_pinmodel_pa_kernel(
                 op0=ALU.subtract,
                 op1=ALU.mult,
             )
-        for g in range(N_BANKS):
-            for half in range(2):
-                zT_ps = work.tile([P, 2, P], F32, tag="work")
-                for e in range(2):
-                    t = 2 * half + e
-                    nc.tensor.transpose(out=zT_ps[:, e, :], in_=z[:, g, t, :], identity=ident_f32[:])
-                for e in range(2):
-                    t = 2 * half + e
-                    k = g * PACK + t
-                    if half == 0:
-                        nc.scalar.activation(
-                            out=y_planes[:, g, t, :],
-                            in_=zT_ps[:, e, :],
-                            func=ACT.Identity,
-                            bias=gain_bias[:, 1, k : k + 1],
-                            scale=gain_bias[:, 0, k : k + 1],
-                        )
-                    else:
-                        nc.vector.tensor_scalar(
-                            out=y_planes[:, g, t, :],
-                            in0=zT_ps[:, e, :],
-                            scalar1=gain_bias[:, 0, k : k + 1],
-                            scalar2=gain_bias[:, 1, k : k + 1],
-                            op0=ALU.mult,
-                            op1=ALU.add,
-                        )
-        for g in range(N_BANKS):
-            regroup(nc.vector.tensor_copy, y_grouped[:, g, :, :], y_planes[:, g, :, :])
-        for g in range(N_BANKS):
+            zT_ps = work.tile([P, PACK, P], F32, tag="work")
+            for t in range(PACK):
+                nc.tensor.transpose(out=zT_ps[:, t, :], in_=z[:, g, t, :], identity=ident_f32[:])
+            for t in range(PACK):
+                k = g * PACK + t
+                nc.scalar.activation(
+                    out=y_planes[:, g, t, :],
+                    in_=zT_ps[:, t, :],
+                    func=ACT.Identity,
+                    bias=gain_bias[:, 1, k : k + 1],
+                    scale=gain_bias[:, 0, k : k + 1],
+                )
+
+        out_ps = acc_pool.tile([P, OUT], F32, name="out_ps", tag="acc0")
+
+        def multiply_y(g):
             nc.vector.quantize_mx(
                 out=y_codes[:, g, :].bitcast(FP8X4),
                 scales=y_scales[:, g, :],
                 in_=y_grouped[:, g, :, :].rearrange("p r t -> p (r t)"),
             )
-        out_ps = work.tile([P, OUT], F32, tag="work")
-        for g in range(N_BANKS):
             nc.tensor.matmul_mx(
                 out=out_ps[:],
                 lhsT=y_codes[:, g, :].bitcast(FP8X4),
@@ -245,6 +292,12 @@ def tile_pinmodel_pa_kernel(
                 start=(g == 0),
                 stop=(g == N_BANKS - 1),
             )
+
+        for g in range(N_BANKS):
+            regroup(nc.vector.tensor_copy, y_grouped[:, g, :, :], y_planes[:, g, :, :])
+            if g > 0:
+                multiply_y(g - 1)
+        multiply_y(N_BANKS - 1)
         out_sb = keep.tile([P, OUT], F32)
         nc.vector.tensor_tensor(out=out_sb[:], in0=out_ps[:], in1=fc_b_all[:], op=ALU.add)
         nc.sync.dma_start(out=out.rearrange("b o n -> b (o n)"), in_=out_sb[:])

@@ -30,7 +30,7 @@ FLOPS = 2 * P * (K1 + 2 * KR) * DIM + 2 * P * DIM * OUT
 
 
 PIECES = ((512, 512, 1024), (1024, 1024), (1024, 1024), (1024, 512, 512))
-VECTOR_COLS = (320, 256, 256, 128)
+VECTOR_COLS = (320, 288, 288, 224)
 
 
 def regroup(copy, grouped, rows):

@@ -25,12 +25,13 @@ CORE_PASSES = KR // K_PASS
 PASSES = 2 * CORE_PASSES
 RUN = 4
 EPS = 1e-5
+VECTOR_HALVES = ((0, 1),)
 
 FLOPS = 2 * P * (K1 + 2 * KR) * DIM + 2 * P * DIM * OUT
 
 
-PIECES = ((512, 512, 1024), (1024, 1024), (1024, 1024), (1024, 512, 512))
-VECTOR_COLS = (320, 288, 288, 224)
+PIECES = ((512, 512, 512, 512), (1024, 1024), (1024, 1024), (1024, 512, 512))
+VECTOR_COLS = (272, 256, 256, 256)
 
 
 def regroup(copy, grouped, rows):
@@ -64,7 +65,7 @@ def tile_pinmodel_pa_kernel(
         w_planes = keep.tile([P, OUT], U8, align_bytes=64)
         nc.vector.memset(w_planes[:].bitcast(I32), 0)
         warm = keep.tile([P, 1], F32)
-        nc.scalar.sqrt(out=warm[:], in_=eps[:])
+        nc.scalar.activation(out=warm[:], in_=eps[:], func=ACT.Abs_reciprocal_sqrt)
 
         cores = [t.rearrange("p q n -> (p q) n") for t in (core2, core3)]
         raw = {}
@@ -86,18 +87,21 @@ def tile_pinmodel_pa_kernel(
         t_sb = [keep.tile([P, KR], BF16, name="t_sb%d" % i) for i in range(2)]
         km1_sb = keep.tile([P, DIM], BF16)
         load_core(0, 0)
-        nc.sync.dma_start(out=x_sb[:], in_=x.rearrange("b i j -> b (i j)"))
-        nc.sync.dma_start(out=t_sb[0][:], in_=t2.rearrange("b p q -> b (p q)"))
         load_core(0, 1)
-        nc.sync.dma_start(out=km1_sb[:], in_=km1.rearrange("i j n -> (i j) n"))
-        nc.sync.dma_start(out=b1_rows[0:1, :], in_=b1.unsqueeze(0))
+        nc.sync.dma_start(out=t_sb[0][:], in_=t2.rearrange("b p q -> b (p q)"))
         load_core(0, 2)
+        load_core(0, 3)
         load_core(1, 0)
-        nc.sync.dma_start(out=t_sb[1][:], in_=t3.rearrange("b p q -> b (p q)"))
         load_core(1, 1)
-        for c in (2, 3):
-            for piece in range(len(PIECES[c])):
-                load_core(c, piece)
+        load_core(2, 0)
+        nc.sync.dma_start(out=t_sb[1][:], in_=t3.rearrange("b p q -> b (p q)"))
+        nc.sync.dma_start(out=x_sb[:], in_=x.rearrange("b i j -> b (i j)"))
+        load_core(2, 1)
+        load_core(3, 0)
+        nc.sync.dma_start(out=b1_rows[0:1, :], in_=b1.unsqueeze(0))
+        nc.sync.dma_start(out=km1_sb[:], in_=km1.rearrange("i j n -> (i j) n"))
+        load_core(3, 1)
+        load_core(3, 2)
         gain_bias_bf16 = keep.tile([P, 2, N_BANKS * PACK], BF16)
         with nc.allow_non_contiguous_dma(reason="two vectors of 2048, in pieces of 8 bytes"):
             for i, vec in enumerate((ln_g, ln_b)):
@@ -126,7 +130,10 @@ def tile_pinmodel_pa_kernel(
         acc = [acc_pool.tile([P, BANK], F32, name="acc%d" % g) for g in range(N_BANKS)]
         o1 = keep.tile([P, N_BANKS, PACK, P], F32)
         o = keep.tile([P, N_BANKS, PACK, P], F32)
-        stats = keep.tile([P, N_BANKS, 6], F32)
+        stats = keep.tile([P, N_BANKS + 1, 3], F32)
+        nc.vector.memset(stats[:], float(BANK))
+        sums = keep.tile([P, N_BANKS], F32)
+        squares = keep.tile([P, BANK], F32)
         xT = keep.tile([P, P], BF16)
         grouped = {}
 
@@ -137,13 +144,16 @@ def tile_pinmodel_pa_kernel(
             regroup(nc.scalar.copy, tile[:, split:, :], raw[(c, g)][:, :, split:])
             grouped[(c, g)] = tile
 
-        def multiply_bank(c, g):
+        def quantize_bank(c, g):
             cols = slice(g * BANK, (g + 1) * BANK)
             nc.vector.quantize_mx(
                 out=c_codes[:, c, cols].bitcast(FP8X4),
                 scales=c_scales[:, c, cols],
                 in_=grouped[(c, g)][:].rearrange("p w j -> p (w j)"),
             )
+
+        def multiply_bank(c, g):
+            cols = slice(g * BANK, (g + 1) * BANK)
             nc.tensor.matmul_mx(
                 out=acc[g][:],
                 lhsT=t_codes[:, c, :].bitcast(FP8X4),
@@ -197,62 +207,89 @@ def tile_pinmodel_pa_kernel(
             nc.scalar.copy(out=o1[:, g, :, :], in_=o1_ps[g][:].rearrange("r (p t) -> r t p", t=PACK))
 
         def add_orders(g):
-            nc.vector.tensor_tensor(
+            nc.vector.scalar_tensor_tensor(
                 out=o[:, g, :, :],
                 in0=acc[g][:].rearrange("r (p t) -> r t p", t=PACK),
+                scalar=1.0,
                 in1=o1[:, g, :, :],
-                op=ALU.add,
+                op0=ALU.mult,
+                op1=ALU.add,
+                accum_out=sums[:, g : g + 1],
             )
 
-        def row_stats(g):
-            nc.vector.bn_stats(out=stats[:, g, :], in_=o[:, g, :, :].rearrange("r t p -> r (t p)"))
+        def bank_mean(g):
+            nc.vector.tensor_scalar(
+                out=stats[:, g, 1:2], in0=sums[:, g : g + 1], scalar1=1.0 / BANK, scalar2=None, op0=ALU.mult
+            )
+
+        def bank_squares(g):
+            nc.scalar.activation(
+                out=squares[:],
+                in_=o[:, g, :, :].rearrange("r t p -> r (t p)"),
+                func=ACT.Square,
+                bias=stats[:, g, 1:2],
+                scale=-1.0,
+                accum_out=stats[:, g, 2:3],
+            )
 
         steps = [(c, g) for c in range(PASSES) for g in range(N_BANKS)]
         last = len(steps) - 1
         regroup_bank(*steps[0])
         for i, (c, g) in enumerate(steps):
+            if i == 1:
+                transpose_t(0)
             if i < last:
                 regroup_bank(*steps[i + 1])
-            if i == 0:
-                transpose_x()
-                transpose_t(0)
+            if i == 2:
                 quantize_t(0)
+            if i == 10:
+                transpose_t(1)
+                transpose_x()
+            if i == 11:
+                quantize_t(1)
+            if i == 13:
                 order_1(0)
                 order_1(1)
-                keep_order_1(0)
-            if 1 <= i < N_BANKS:
-                keep_order_1(i)
-                if i + 1 < N_BANKS:
-                    order_1(i + 1)
-            if i == 5:
-                transpose_t(1)
-            if i == 6:
-                quantize_t(1)
-            multiply_bank(c, g)
-            if i >= last - 1:
-                add_orders(i - last + 1)
-            if i == last:
-                row_stats(0)
-        add_orders(2)
-        row_stats(1)
-        add_orders(3)
-        row_stats(2)
-        row_stats(3)
+            if i == 14:
+                order_1(2)
+                order_1(3)
+            quantize_bank(c, g)
+            if i == 2:
+                for j in range(3):
+                    multiply_bank(*steps[j])
+            elif i == 11:
+                for j in range(8, 12):
+                    multiply_bank(*steps[j])
+            elif i > 2 and not 8 <= i < 11:
+                multiply_bank(c, g)
+        for g in range(N_BANKS):
+            keep_order_1(g)
+            add_orders(g)
+            if g > 0:
+                bank_mean(g - 1)
+        for g in range(N_BANKS - 1):
+            bank_squares(g)
+        nc.vector.bn_stats(
+            out=stats[:, N_BANKS - 1 :, :].rearrange("r g s -> r (g s)"),
+            in_=o[:, N_BANKS - 1, :, :].rearrange("r t p -> r (t p)"),
+        )
 
         gain_bias = keep.tile([P, 2, N_BANKS * PACK], F32)
         nc.scalar.copy(out=gain_bias[:], in_=gain_bias_bf16[:])
         mean_var = keep.tile([P, 2], F32)
         nc.vector.bn_aggr(out=mean_var[:], in_=stats[:].rearrange("r g s -> r (g s)"))
-        std = keep.tile([P, 1], F32)
-        nc.scalar.activation(out=std[:], in_=mean_var[:, 1:2], func=ACT.Sqrt, bias=eps[:], scale=1.0)
         rstd = keep.tile([P, 1], F32)
-        nc.vector.reciprocal(out=rstd[:], in_=std[:])
+        nc.scalar.activation(
+            out=rstd[:], in_=mean_var[:, 1:2], func=ACT.Abs_reciprocal_sqrt, bias=eps[:], scale=1.0
+        )
 
         z = keep.tile([P, N_BANKS, PACK, P], F32)
         y_planes = keep.tile([P, N_BANKS, PACK, P], BF16)
         y_grouped = keep.tile([P, N_BANKS, P, PACK], BF16, align_bytes=64)
         y_codes = keep.tile([P, N_BANKS, P], U32, align_bytes=64)
         y_scales = keep.tile([P, N_BANKS, P], U8, align_bytes=64)
+        vector_halves = []
+        z_banks = [(work, "work")] * 4 + [(acc_pool, "acc%d" % g) for g in range(1, N_BANKS)] + [(work, "work")]
         for g in range(N_BANKS):
             nc.vector.tensor_scalar(
                 out=z[:, g, :, :],
@@ -262,17 +299,36 @@ def tile_pinmodel_pa_kernel(
                 op0=ALU.subtract,
                 op1=ALU.mult,
             )
-            zT_ps = work.tile([P, PACK, P], F32, tag="work")
-            for t in range(PACK):
-                nc.tensor.transpose(out=zT_ps[:, t, :], in_=z[:, g, t, :], identity=ident_f32[:])
-            for t in range(PACK):
+            for half in range(2):
+                pool, tag = z_banks[2 * g + half]
+                zT_ps = pool.tile([P, 2, P], F32, name="zT_ps", tag=tag)
+                for e in range(2):
+                    nc.tensor.transpose(out=zT_ps[:, e, :], in_=z[:, g, 2 * half + e, :], identity=ident_f32[:])
+                for e in range(2):
+                    t = 2 * half + e
+                    k = g * PACK + t
+                    if (g, half) in VECTOR_HALVES:
+                        continue
+                    nc.scalar.activation(
+                        out=y_planes[:, g, t, :],
+                        in_=zT_ps[:, e, :],
+                        func=ACT.Identity,
+                        bias=gain_bias[:, 1, k : k + 1],
+                        scale=gain_bias[:, 0, k : k + 1],
+                    )
+                if (g, half) in VECTOR_HALVES:
+                    vector_halves.append((g, half, zT_ps))
+        for g, half, zT_ps in vector_halves:
+            for e in range(2):
+                t = 2 * half + e
                 k = g * PACK + t
-                nc.scalar.activation(
+                nc.vector.tensor_scalar(
                     out=y_planes[:, g, t, :],
-                    in_=zT_ps[:, t, :],
-                    func=ACT.Identity,
-                    bias=gain_bias[:, 1, k : k + 1],
-                    scale=gain_bias[:, 0, k : k + 1],
+                    in0=zT_ps[:, e, :],
+                    scalar1=gain_bias[:, 0, k : k + 1],
+                    scalar2=gain_bias[:, 1, k : k + 1],
+                    op0=ALU.mult,
+                    op1=ALU.add,
                 )
 
         out_ps = acc_pool.tile([P, OUT], F32, name="out_ps", tag="acc0")
@@ -299,5 +355,7 @@ def tile_pinmodel_pa_kernel(
                 multiply_y(g - 1)
         multiply_y(N_BANKS - 1)
         out_sb = keep.tile([P, OUT], F32)
-        nc.vector.tensor_tensor(out=out_sb[:], in0=out_ps[:], in1=fc_b_all[:], op=ALU.add)
-        nc.sync.dma_start(out=out.rearrange("b o n -> b (o n)"), in_=out_sb[:])
+        for h in range(2):
+            cols = slice(h * OUT // 2, (h + 1) * OUT // 2)
+            nc.vector.tensor_tensor(out=out_sb[:, cols], in0=out_ps[:, cols], in1=fc_b_all[:, cols], op=ALU.add)
+            nc.sync.dma_start(out=out.rearrange("b o n -> b (o n)")[:, cols], in_=out_sb[:, cols])

@@ -30,7 +30,7 @@ VECTOR_HALVES = ((0, 1),)
 FLOPS = 2 * P * (K1 + 2 * KR) * DIM + 2 * P * DIM * OUT
 
 
-PIECES = ((512, 512, 512, 512), (1024, 1024), (1024, 1024), (1024, 512, 512))
+PIECES = ((1024, 1024), (2048,), (2048,), (1024, 1024))
 VECTOR_COLS = (272, 256, 256, 256)
 
 
@@ -88,20 +88,15 @@ def tile_pinmodel_pa_kernel(
         km1_sb = keep.tile([P, DIM], BF16)
         load_core(0, 0)
         load_core(0, 1)
-        nc.sync.dma_start(out=t_sb[0][:], in_=t2.rearrange("b p q -> b (p q)"))
-        load_core(0, 2)
-        load_core(0, 3)
         load_core(1, 0)
-        load_core(1, 1)
+        nc.sync.dma_start(out=t_sb[0][:], in_=t2.rearrange("b p q -> b (p q)"))
         load_core(2, 0)
         nc.sync.dma_start(out=t_sb[1][:], in_=t3.rearrange("b p q -> b (p q)"))
         nc.sync.dma_start(out=x_sb[:], in_=x.rearrange("b i j -> b (i j)"))
-        load_core(2, 1)
-        load_core(3, 0)
         nc.sync.dma_start(out=b1_rows[0:1, :], in_=b1.unsqueeze(0))
         nc.sync.dma_start(out=km1_sb[:], in_=km1.rearrange("i j n -> (i j) n"))
+        load_core(3, 0)
         load_core(3, 1)
-        load_core(3, 2)
         gain_bias_bf16 = keep.tile([P, 2, N_BANKS * PACK], BF16)
         with nc.allow_non_contiguous_dma(reason="two vectors of 2048, in pieces of 8 bytes"):
             for i, vec in enumerate((ln_g, ln_b)):
@@ -133,7 +128,7 @@ def tile_pinmodel_pa_kernel(
         stats = keep.tile([P, N_BANKS + 1, 3], F32)
         nc.vector.memset(stats[:], float(BANK))
         sums = keep.tile([P, N_BANKS], F32)
-        squares = keep.tile([P, BANK], F32)
+        squares = keep.tile([P, N_BANKS, BANK], BF16)
         xT = keep.tile([P, P], BF16)
         grouped = {}
 
@@ -224,7 +219,7 @@ def tile_pinmodel_pa_kernel(
 
         def bank_squares(g):
             nc.scalar.activation(
-                out=squares[:],
+                out=squares[:, g, :],
                 in_=o[:, g, :, :].rearrange("r t p -> r (t p)"),
                 func=ACT.Square,
                 bias=stats[:, g, 1:2],
@@ -236,31 +231,27 @@ def tile_pinmodel_pa_kernel(
         last = len(steps) - 1
         regroup_bank(*steps[0])
         for i, (c, g) in enumerate(steps):
-            if i == 1:
+            if i == 4:
                 transpose_t(0)
-            if i < last:
-                regroup_bank(*steps[i + 1])
-            if i == 2:
-                quantize_t(0)
             if i == 10:
                 transpose_t(1)
                 transpose_x()
+            if i < last:
+                regroup_bank(*steps[i + 1])
+            if i == 5:
+                quantize_t(0)
             if i == 11:
                 quantize_t(1)
-            if i == 13:
-                order_1(0)
-                order_1(1)
-            if i == 14:
-                order_1(2)
-                order_1(3)
+                for j in range(N_BANKS):
+                    order_1(j)
             quantize_bank(c, g)
-            if i == 2:
-                for j in range(3):
+            if i == 5:
+                for j in range(6):
                     multiply_bank(*steps[j])
             elif i == 11:
                 for j in range(8, 12):
                     multiply_bank(*steps[j])
-            elif i > 2 and not 8 <= i < 11:
+            elif i > 5 and not 8 <= i < 11:
                 multiply_bank(c, g)
         for g in range(N_BANKS):
             keep_order_1(g)

@@ -25,13 +25,12 @@ CORE_PASSES = KR // K_PASS
 PASSES = 2 * CORE_PASSES
 RUN = 4
 EPS = 1e-5
-VECTOR_HALVES = ((0, 1),)
 
 FLOPS = 2 * P * (K1 + 2 * KR) * DIM + 2 * P * DIM * OUT
 
 
 PIECES = ((1024, 1024), (2048,), (2048,), (1024, 1024))
-VECTOR_COLS = (272, 256, 256, 256)
+VECTOR_COLS = (256, 256, 256, 256)
 
 
 def regroup(copy, grouped, rows):
@@ -159,10 +158,15 @@ def tile_pinmodel_pa_kernel(
                 stop=(c == PASSES - 1),
             )
 
+        in_psum = {}
+
         def transpose_x():
             xT_ps = work.tile([P, P], BF16, tag="work")
             nc.tensor.transpose(out=xT_ps[:], in_=x_sb[:], identity=ident_bf16[:])
-            nc.scalar.copy(out=xT[:], in_=xT_ps[:])
+            in_psum["x"] = xT_ps
+
+        def keep_x():
+            nc.scalar.copy(out=xT[:], in_=in_psum["x"][:])
 
         t_grouped = {}
 
@@ -176,10 +180,13 @@ def tile_pinmodel_pa_kernel(
                         in_=words[:, g * K_PASS // 2 + u : (g + 1) * K_PASS // 2 : 2],
                         identity=ident_f32[:],
                     )
+            in_psum[i] = tT_ps
+
+        def keep_t(i):
             t_grouped[i] = keep.tile([P, KR], BF16, name="t_grouped%d" % i, align_bytes=64)
             nc.scalar.copy(
                 out=t_grouped[i][:].bitcast(F32).rearrange("p (g r u) -> p g r u", g=CORE_PASSES, u=2),
-                in_=tT_ps[:].rearrange("p g u r -> p g r u"),
+                in_=in_psum[i][:].rearrange("p g u r -> p g r u"),
             )
 
         def quantize_t(i):
@@ -233,14 +240,19 @@ def tile_pinmodel_pa_kernel(
         for i, (c, g) in enumerate(steps):
             if i == 4:
                 transpose_t(0)
-            if i == 10:
+            if i == 9:
                 transpose_t(1)
                 transpose_x()
             if i < last:
                 regroup_bank(*steps[i + 1])
+            if i == 4:
+                keep_t(0)
+            if i == 9:
+                keep_t(1)
+                keep_x()
             if i == 5:
                 quantize_t(0)
-            if i == 11:
+            if i == 10:
                 quantize_t(1)
                 for j in range(N_BANKS):
                     order_1(j)
@@ -248,10 +260,10 @@ def tile_pinmodel_pa_kernel(
             if i == 5:
                 for j in range(6):
                     multiply_bank(*steps[j])
-            elif i == 11:
-                for j in range(8, 12):
+            elif i == 10:
+                for j in range(8, 11):
                     multiply_bank(*steps[j])
-            elif i > 5 and not 8 <= i < 11:
+            elif i > 5 and not 8 <= i < 10:
                 multiply_bank(c, g)
         for g in range(N_BANKS):
             keep_order_1(g)
@@ -279,9 +291,11 @@ def tile_pinmodel_pa_kernel(
         y_grouped = keep.tile([P, N_BANKS, P, PACK], BF16, align_bytes=64)
         y_codes = keep.tile([P, N_BANKS, P], U32, align_bytes=64)
         y_scales = keep.tile([P, N_BANKS, P], U8, align_bytes=64)
-        vector_halves = []
         z_banks = [(work, "work")] * 4 + [(acc_pool, "acc%d" % g) for g in range(1, N_BANKS)] + [(work, "work")]
-        for g in range(N_BANKS):
+        zT = {}
+        out_ps = acc_pool.tile([P, OUT], F32, name="out_ps", tag="acc0")
+
+        def normalise(g):
             nc.vector.tensor_scalar(
                 out=z[:, g, :, :],
                 in0=o[:, g, :, :],
@@ -290,39 +304,41 @@ def tile_pinmodel_pa_kernel(
                 op0=ALU.subtract,
                 op1=ALU.mult,
             )
-            for half in range(2):
-                pool, tag = z_banks[2 * g + half]
-                zT_ps = pool.tile([P, 2, P], F32, name="zT_ps", tag=tag)
-                for e in range(2):
-                    nc.tensor.transpose(out=zT_ps[:, e, :], in_=z[:, g, 2 * half + e, :], identity=ident_f32[:])
-                for e in range(2):
-                    t = 2 * half + e
-                    k = g * PACK + t
-                    if (g, half) in VECTOR_HALVES:
-                        continue
-                    nc.scalar.activation(
-                        out=y_planes[:, g, t, :],
-                        in_=zT_ps[:, e, :],
-                        func=ACT.Identity,
-                        bias=gain_bias[:, 1, k : k + 1],
-                        scale=gain_bias[:, 0, k : k + 1],
-                    )
-                if (g, half) in VECTOR_HALVES:
-                    vector_halves.append((g, half, zT_ps))
-        for g, half, zT_ps in vector_halves:
+
+        def transpose_z(g, half):
+            pool, tag = z_banks[2 * g + half]
+            zT[(g, half)] = pool.tile([P, 2, P], F32, name="zT_ps", tag=tag)
+            for e in range(2):
+                nc.tensor.transpose(
+                    out=zT[(g, half)][:, e, :], in_=z[:, g, 2 * half + e, :], identity=ident_f32[:]
+                )
+
+        def apply_gain(g, half, on_vector):
             for e in range(2):
                 t = 2 * half + e
                 k = g * PACK + t
-                nc.vector.tensor_scalar(
-                    out=y_planes[:, g, t, :],
-                    in0=zT_ps[:, e, :],
-                    scalar1=gain_bias[:, 0, k : k + 1],
-                    scalar2=gain_bias[:, 1, k : k + 1],
-                    op0=ALU.mult,
-                    op1=ALU.add,
-                )
+                gain = gain_bias[:, 0, k : k + 1]
+                bias = gain_bias[:, 1, k : k + 1]
+                if on_vector:
+                    nc.vector.tensor_scalar(
+                        out=y_planes[:, g, t, :],
+                        in0=zT[(g, half)][:, e, :],
+                        scalar1=gain,
+                        scalar2=bias,
+                        op0=ALU.mult,
+                        op1=ALU.add,
+                    )
+                else:
+                    nc.scalar.activation(
+                        out=y_planes[:, g, t, :],
+                        in_=zT[(g, half)][:, e, :],
+                        func=ACT.Identity,
+                        bias=bias,
+                        scale=gain,
+                    )
 
-        out_ps = acc_pool.tile([P, OUT], F32, name="out_ps", tag="acc0")
+        def regroup_y(g):
+            regroup(nc.vector.tensor_copy, y_grouped[:, g, :, :], y_planes[:, g, :, :])
 
         def multiply_y(g):
             nc.vector.quantize_mx(
@@ -340,11 +356,34 @@ def tile_pinmodel_pa_kernel(
                 stop=(g == N_BANKS - 1),
             )
 
-        for g in range(N_BANKS):
-            regroup(nc.vector.tensor_copy, y_grouped[:, g, :, :], y_planes[:, g, :, :])
-            if g > 0:
-                multiply_y(g - 1)
-        multiply_y(N_BANKS - 1)
+        normalise(0)
+        transpose_z(0, 0)
+        transpose_z(0, 1)
+        normalise(1)
+        transpose_z(1, 0)
+        transpose_z(1, 1)
+        normalise(2)
+        transpose_z(2, 0)
+        transpose_z(2, 1)
+        normalise(3)
+        transpose_z(3, 0)
+        apply_gain(0, 0, False)
+        transpose_z(3, 1)
+        apply_gain(1, 0, False)
+        apply_gain(2, 0, False)
+        apply_gain(2, 1, False)
+        apply_gain(3, 0, False)
+        apply_gain(0, 1, True)
+        regroup_y(0)
+        apply_gain(1, 1, True)
+        regroup_y(1)
+        multiply_y(0)
+        apply_gain(3, 1, True)
+        regroup_y(2)
+        multiply_y(1)
+        regroup_y(3)
+        multiply_y(2)
+        multiply_y(3)
         out_sb = keep.tile([P, OUT], F32)
         for h in range(2):
             cols = slice(h * OUT // 2, (h + 1) * OUT // 2)

@@ -158,6 +158,21 @@ def tile_pinmodel_pa_kernel(
                 stop=(c == PASSES - 1),
             )
 
+        def keep_warm(passes):
+            c, g = steps[-1]
+            cols = slice(g * BANK, (g + 1) * BANK)
+            spare = work.tile([P, BANK], F32, name="spare", tag="work")
+            for repeat in range(passes):
+                nc.tensor.matmul_mx(
+                    out=spare[:],
+                    lhsT=t_codes[:, c, :].bitcast(FP8X4),
+                    lhsT_scale=t_scales[:, c, :],
+                    rhs=c_codes[:, c, cols].bitcast(FP8X4),
+                    rhs_scale=c_scales[:, c, cols],
+                    start=True,
+                    stop=True,
+                )
+
         in_psum = {}
 
         def transpose_x():
@@ -267,6 +282,8 @@ def tile_pinmodel_pa_kernel(
                 multiply_bank(c, g)
         for g in range(N_BANKS):
             keep_order_1(g)
+            if g == 0:
+                keep_warm(14)
             add_orders(g)
             if g > 0:
                 bank_mean(g - 1)
@@ -374,6 +391,7 @@ def tile_pinmodel_pa_kernel(
         apply_gain(2, 1, False)
         apply_gain(3, 0, False)
         apply_gain(0, 1, True)
+        keep_warm(3)
         regroup_y(0)
         apply_gain(1, 1, True)
         regroup_y(1)

@@ -29,7 +29,7 @@ EPS = 1e-5
 FLOPS = 2 * P * (K1 + 2 * KR) * DIM + 2 * P * DIM * OUT
 
 
-PIECES = ((1024, 1024), (2048,), (2048,), (1024, 1024))
+PIECES = ((1024, 1024), (1024, 1024), (1024, 1024), (1024, 512, 512))
 VECTOR_COLS = (256, 256, 256, 256)
 
 
@@ -87,15 +87,18 @@ def tile_pinmodel_pa_kernel(
         km1_sb = keep.tile([P, DIM], BF16)
         load_core(0, 0)
         load_core(0, 1)
-        load_core(1, 0)
         nc.sync.dma_start(out=t_sb[0][:], in_=t2.rearrange("b p q -> b (p q)"))
+        load_core(1, 0)
+        load_core(1, 1)
         load_core(2, 0)
         nc.sync.dma_start(out=t_sb[1][:], in_=t3.rearrange("b p q -> b (p q)"))
         nc.sync.dma_start(out=x_sb[:], in_=x.rearrange("b i j -> b (i j)"))
+        load_core(2, 1)
+        load_core(3, 0)
         nc.sync.dma_start(out=b1_rows[0:1, :], in_=b1.unsqueeze(0))
         nc.sync.dma_start(out=km1_sb[:], in_=km1.rearrange("i j n -> (i j) n"))
-        load_core(3, 0)
         load_core(3, 1)
+        load_core(3, 2)
         gain_bias_bf16 = keep.tile([P, 2, N_BANKS * PACK], BF16)
         with nc.allow_non_contiguous_dma(reason="two vectors of 2048, in pieces of 8 bytes"):
             for i, vec in enumerate((ln_g, ln_b)):
@@ -253,42 +256,42 @@ def tile_pinmodel_pa_kernel(
         last = len(steps) - 1
         regroup_bank(*steps[0])
         for i, (c, g) in enumerate(steps):
-            if i == 4:
+            if i == 3:
                 transpose_t(0)
             if i == 9:
                 transpose_t(1)
                 transpose_x()
             if i < last:
                 regroup_bank(*steps[i + 1])
-            if i == 4:
+            if i == 3:
                 keep_t(0)
             if i == 9:
                 keep_t(1)
                 keep_x()
-            if i == 5:
+            if i == 4:
                 quantize_t(0)
             if i == 10:
                 quantize_t(1)
+            if i == 12:
                 for j in range(N_BANKS):
                     order_1(j)
             quantize_bank(c, g)
-            if i == 5:
-                for j in range(6):
+            if i == 4:
+                for j in range(5):
                     multiply_bank(*steps[j])
             elif i == 10:
                 for j in range(8, 11):
                     multiply_bank(*steps[j])
-            elif i > 5 and not 8 <= i < 10:
+            elif i > 4 and not 8 <= i < 10:
                 multiply_bank(c, g)
         for g in range(N_BANKS):
             keep_order_1(g)
-            if g == 0:
-                keep_warm(14)
+        keep_warm(14)
+        for g in range(N_BANKS):
             add_orders(g)
             if g > 0:
                 bank_mean(g - 1)
-        for g in range(N_BANKS - 1):
-            bank_squares(g)
+                bank_squares(g - 1)
         nc.vector.bn_stats(
             out=stats[:, N_BANKS - 1 :, :].rearrange("r g s -> r (g s)"),
             in_=o[:, N_BANKS - 1, :, :].rearrange("r t p -> r (t p)"),

@@ -234,11 +234,11 @@ def tile_pinmodel_pa_kernel(
                 in1=o1[:, g, :, :],
                 op0=ALU.mult,
                 op1=ALU.add,
-                accum_out=sums[:, g : g + 1],
+                accum_out=sums[:, g : g + 1] if g < N_BANKS - 1 else None,
             )
 
         def bank_mean(g):
-            nc.vector.tensor_scalar(
+            nc.gpsimd.tensor_scalar(
                 out=stats[:, g, 1:2], in0=sums[:, g : g + 1], scalar1=1.0 / BANK, scalar2=None, op0=ALU.mult
             )
 
@@ -393,13 +393,13 @@ def tile_pinmodel_pa_kernel(
         apply_gain(2, 0, False)
         apply_gain(2, 1, False)
         apply_gain(3, 0, False)
+        apply_gain(3, 1, False)
         apply_gain(0, 1, True)
         keep_warm(3)
         regroup_y(0)
         apply_gain(1, 1, True)
         regroup_y(1)
         multiply_y(0)
-        apply_gain(3, 1, True)
         regroup_y(2)
         multiply_y(1)
         regroup_y(3)

@@ -29,7 +29,7 @@ EPS = 1e-5
 FLOPS = 2 * P * (K1 + 2 * KR) * DIM + 2 * P * DIM * OUT
 
 
-PIECES = ((1024, 1024), (1024, 1024), (1024, 1024), (1024, 512, 512))
+PIECES = ((2048,), (2048,), (1024, 1024), (1024, 512, 512))
 VECTOR_COLS = (256, 256, 256, 256)
 
 
@@ -86,10 +86,8 @@ def tile_pinmodel_pa_kernel(
         t_sb = [keep.tile([P, KR], BF16, name="t_sb%d" % i) for i in range(2)]
         km1_sb = keep.tile([P, DIM], BF16)
         load_core(0, 0)
-        load_core(0, 1)
-        nc.sync.dma_start(out=t_sb[0][:], in_=t2.rearrange("b p q -> b (p q)"))
         load_core(1, 0)
-        load_core(1, 1)
+        nc.sync.dma_start(out=t_sb[0][:], in_=t2.rearrange("b p q -> b (p q)"))
         load_core(2, 0)
         nc.sync.dma_start(out=t_sb[1][:], in_=t3.rearrange("b p q -> b (p q)"))
         nc.sync.dma_start(out=x_sb[:], in_=x.rearrange("b i j -> b (i j)"))
@@ -256,19 +254,19 @@ def tile_pinmodel_pa_kernel(
         last = len(steps) - 1
         regroup_bank(*steps[0])
         for i, (c, g) in enumerate(steps):
-            if i == 3:
+            if i == 4:
                 transpose_t(0)
             if i == 9:
                 transpose_t(1)
                 transpose_x()
             if i < last:
                 regroup_bank(*steps[i + 1])
-            if i == 3:
+            if i == 4:
                 keep_t(0)
             if i == 9:
                 keep_t(1)
                 keep_x()
-            if i == 4:
+            if i == 5:
                 quantize_t(0)
             if i == 10:
                 quantize_t(1)
@@ -276,13 +274,13 @@ def tile_pinmodel_pa_kernel(
                 for j in range(N_BANKS):
                     order_1(j)
             quantize_bank(c, g)
-            if i == 4:
-                for j in range(5):
+            if i == 5:
+                for j in range(6):
                     multiply_bank(*steps[j])
             elif i == 10:
                 for j in range(8, 11):
                     multiply_bank(*steps[j])
-            elif i > 4 and not 8 <= i < 10:
+            elif i > 5 and not 8 <= i < 10:
                 multiply_bank(c, g)
         for g in range(N_BANKS):
             keep_order_1(g)

@@ -311,12 +311,11 @@ def tile_pinmodel_pa_kernel(
         y_scales = keep.tile([P, N_BANKS, P], U8, align_bytes=64)
         z_banks = [(work, "work")] * 4 + [(acc_pool, "acc%d" % g) for g in range(1, N_BANKS)] + [(work, "work")]
         zT = {}
-        out_ps = acc_pool.tile([P, OUT], F32, name="out_ps", tag="acc0")
 
-        def normalise(g):
+        def normalise(g, first=0, last=PACK):
             nc.vector.tensor_scalar(
-                out=z[:, g, :, :],
-                in0=o[:, g, :, :],
+                out=z[:, g, first:last, :],
+                in0=o[:, g, first:last, :],
                 scalar1=mean_var[:, 0:1],
                 scalar2=rstd[:],
                 op0=ALU.subtract,
@@ -364,18 +363,21 @@ def tile_pinmodel_pa_kernel(
                 scales=y_scales[:, g, :],
                 in_=y_grouped[:, g, :, :].rearrange("p r t -> p (r t)"),
             )
-            nc.tensor.matmul_mx(
-                out=out_ps[:],
-                lhsT=y_codes[:, g, :].bitcast(FP8X4),
-                lhsT_scale=y_scales[:, g, :],
-                rhs=w_words[:, g, :].bitcast(FP8X4),
-                rhs_scale=w_planes[PACK * g : P, :],
-                start=(g == 0),
-                stop=(g == N_BANKS - 1),
-            )
+            for h in range(2):
+                cols = slice(h * OUT // 2, (h + 1) * OUT // 2)
+                nc.tensor.matmul_mx(
+                    out=out_ps[h][:],
+                    lhsT=y_codes[:, g, :].bitcast(FP8X4),
+                    lhsT_scale=y_scales[:, g, :],
+                    rhs=w_words[:, g, cols].bitcast(FP8X4),
+                    rhs_scale=w_planes[PACK * g : P, cols],
+                    start=(g == 0),
+                    stop=(g == N_BANKS - 1),
+                )
 
-        normalise(0)
+        normalise(0, 0, 2)
         transpose_z(0, 0)
+        normalise(0, 2, 4)
         transpose_z(0, 1)
         normalise(1)
         transpose_z(1, 0)
@@ -388,14 +390,18 @@ def tile_pinmodel_pa_kernel(
         apply_gain(0, 0, False)
         transpose_z(3, 1)
         apply_gain(1, 0, False)
+        apply_gain(1, 1, False)
         apply_gain(2, 0, False)
         apply_gain(2, 1, False)
         apply_gain(3, 0, False)
         apply_gain(3, 1, False)
         apply_gain(0, 1, True)
         keep_warm(3)
+        out_ps = [
+            acc_pool.tile([P, OUT // 2], F32, name="out_ps0", tag="acc0"),
+            work.tile([P, OUT // 2], F32, name="out_ps1", tag="work"),
+        ]
         regroup_y(0)
-        apply_gain(1, 1, True)
         regroup_y(1)
         multiply_y(0)
         regroup_y(2)
@@ -406,5 +412,5 @@ def tile_pinmodel_pa_kernel(
         out_sb = keep.tile([P, OUT], F32)
         for h in range(2):
             cols = slice(h * OUT // 2, (h + 1) * OUT // 2)
-            nc.vector.tensor_tensor(out=out_sb[:, cols], in0=out_ps[:, cols], in1=fc_b_all[:, cols], op=ALU.add)
+            nc.vector.tensor_tensor(out=out_sb[:, cols], in0=out_ps[h][:], in1=fc_b_all[:, cols], op=ALU.add)
             nc.sync.dma_start(out=out.rearrange("b o n -> b (o n)")[:, cols], in_=out_sb[:, cols])

@@ -29,8 +29,8 @@ EPS = 1e-5
 FLOPS = 2 * P * (K1 + 2 * KR) * DIM + 2 * P * DIM * OUT
 
 
-PIECES = ((2048,), (2048,), (1024, 1024), (1024, 512, 512))
-VECTOR_COLS = (256, 256, 256, 256)
+PIECES = ((1024,1024),(1024,1024),(1024,1024),(1024,512,512))
+VECTOR_COLS = (256,256,256,256)
 
 
 def regroup(copy, grouped, rows):
@@ -85,18 +85,20 @@ def tile_pinmodel_pa_kernel(
         x_sb = keep.tile([P, K1], BF16)
         t_sb = [keep.tile([P, KR], BF16, name="t_sb%d" % i) for i in range(2)]
         km1_sb = keep.tile([P, DIM], BF16)
-        load_core(0, 0)
-        load_core(1, 0)
+        load_core(0,0)
+        load_core(0,1)
+        load_core(1,0)
         nc.sync.dma_start(out=t_sb[0][:], in_=t2.rearrange("b p q -> b (p q)"))
-        load_core(2, 0)
+        load_core(1,1)
         nc.sync.dma_start(out=t_sb[1][:], in_=t3.rearrange("b p q -> b (p q)"))
+        load_core(2,0)
         nc.sync.dma_start(out=x_sb[:], in_=x.rearrange("b i j -> b (i j)"))
-        load_core(2, 1)
-        load_core(3, 0)
-        nc.sync.dma_start(out=b1_rows[0:1, :], in_=b1.unsqueeze(0))
+        load_core(3,0)
         nc.sync.dma_start(out=km1_sb[:], in_=km1.rearrange("i j n -> (i j) n"))
-        load_core(3, 1)
-        load_core(3, 2)
+        nc.sync.dma_start(out=b1_rows[0:1, :], in_=b1.unsqueeze(0))
+        load_core(2,1)
+        load_core(3,1)
+        load_core(3,2)
         gain_bias_bf16 = keep.tile([P, 2, N_BANKS * PACK], BF16)
         with nc.allow_non_contiguous_dma(reason="two vectors of 2048, in pieces of 8 bytes"):
             for i, vec in enumerate((ln_g, ln_b)):
@@ -160,7 +162,7 @@ def tile_pinmodel_pa_kernel(
             )
 
         def keep_warm(passes):
-            c, g = steps[-1]
+            c, g = 3, 3
             cols = slice(g * BANK, (g + 1) * BANK)
             spare = work.tile([P, BANK], F32, name="spare", tag="work")
             for repeat in range(passes):
@@ -250,46 +252,81 @@ def tile_pinmodel_pa_kernel(
                 accum_out=stats[:, g, 2:3],
             )
 
-        steps = [(c, g) for c in range(PASSES) for g in range(N_BANKS)]
-        last = len(steps) - 1
-        regroup_bank(*steps[0])
-        for i, (c, g) in enumerate(steps):
-            if i == 4:
-                transpose_t(0)
-            if i == 9:
-                transpose_t(1)
-                transpose_x()
-            if i < last:
-                regroup_bank(*steps[i + 1])
-            if i == 4:
-                keep_t(0)
-            if i == 9:
-                keep_t(1)
-                keep_x()
-            if i == 5:
-                quantize_t(0)
-            if i == 10:
-                quantize_t(1)
-            if i == 12:
-                for j in range(N_BANKS):
-                    order_1(j)
-            quantize_bank(c, g)
-            if i == 5:
-                for j in range(6):
-                    multiply_bank(*steps[j])
-            elif i == 10:
-                for j in range(8, 11):
-                    multiply_bank(*steps[j])
-            elif i > 5 and not 8 <= i < 10:
-                multiply_bank(c, g)
-        for g in range(N_BANKS):
-            keep_order_1(g)
-        keep_warm(14)
-        for g in range(N_BANKS):
-            add_orders(g)
-            if g > 0:
-                bank_mean(g - 1)
-                bank_squares(g - 1)
+        regroup_bank(0, 0)
+        regroup_bank(0, 1)
+        quantize_bank(0, 0)
+        regroup_bank(0, 2)
+        quantize_bank(0, 1)
+        regroup_bank(0, 3)
+        quantize_bank(0, 2)
+        regroup_bank(1, 0)
+        quantize_bank(0, 3)
+        transpose_t(0)
+        regroup_bank(1, 1)
+        quantize_bank(1, 0)
+        keep_t(0)
+        regroup_bank(1, 2)
+        quantize_bank(1, 1)
+        quantize_t(0)
+        transpose_t(1)
+        regroup_bank(1, 3)
+        multiply_bank(0, 0)
+        multiply_bank(0, 1)
+        multiply_bank(0, 2)
+        multiply_bank(0, 3)
+        multiply_bank(1, 0)
+        multiply_bank(1, 1)
+        keep_t(1)
+        quantize_bank(1, 2)
+        multiply_bank(1, 2)
+        quantize_t(1)
+        regroup_bank(2, 0)
+        quantize_bank(1, 3)
+        multiply_bank(1, 3)
+        transpose_x()
+        regroup_bank(2, 1)
+        keep_x()
+        quantize_bank(2, 0)
+        multiply_bank(2, 0)
+        regroup_bank(3, 0)
+        quantize_bank(2, 1)
+        multiply_bank(2, 1)
+        order_1(0)
+        order_1(1)
+        regroup_bank(3, 1)
+        quantize_bank(3, 0)
+        multiply_bank(3, 0)
+        keep_order_1(0)
+        keep_order_1(1)
+        order_1(2)
+        order_1(3)
+        quantize_bank(3, 1)
+        multiply_bank(3, 1)
+        add_orders(0)
+        regroup_bank(2, 2)
+        regroup_bank(2, 3)
+        quantize_bank(2, 2)
+        multiply_bank(2, 2)
+        regroup_bank(3, 2)
+        quantize_bank(2, 3)
+        multiply_bank(2, 3)
+        regroup_bank(3, 3)
+        keep_order_1(2)
+        keep_order_1(3)
+        quantize_bank(3, 2)
+        multiply_bank(3, 2)
+        add_orders(1)
+        quantize_bank(3, 3)
+        multiply_bank(3, 3)
+        keep_warm(8)
+        bank_mean(0)
+        bank_squares(0)
+        bank_mean(1)
+        bank_squares(1)
+        add_orders(2)
+        bank_mean(2)
+        bank_squares(2)
+        add_orders(3)
         nc.vector.bn_stats(
             out=stats[:, N_BANKS - 1 :, :].rearrange("r g s -> r (g s)"),
             in_=o[:, N_BANKS - 1, :, :].rearrange("r t p -> r (t p)"),

@@ -48,7 +48,8 @@ def tile_pinmodel_pa_kernel(
         keep = ctx.enter_context(tc.tile_pool(name="keep", bufs=1))
         grouped_pool = ctx.enter_context(tc.tile_pool(name="grouped", bufs=4))
         acc_pool = ctx.enter_context(tc.psum_pool(name="acc", bufs=1))
-        work = ctx.enter_context(tc.psum_pool(name="work", bufs=4))
+        work = ctx.enter_context(tc.psum_pool(name="work", bufs=3))
+        spare_pool = ctx.enter_context(tc.psum_pool(name="spare", bufs=1))
         ctx.enter_context(tc.manual_schedule())
 
         b1_rows = keep.tile([P, DIM], BF16)
@@ -85,19 +86,19 @@ def tile_pinmodel_pa_kernel(
         x_sb = keep.tile([P, K1], BF16)
         t_sb = [keep.tile([P, KR], BF16, name="t_sb%d" % i) for i in range(2)]
         km1_sb = keep.tile([P, DIM], BF16)
+        nc.sync.dma_start(out=t_sb[0][:], in_=t2.rearrange("b p q -> b (p q)"))
+        nc.sync.dma_start(out=t_sb[1][:], in_=t3.rearrange("b p q -> b (p q)"))
+        nc.sync.dma_start(out=x_sb[:], in_=x.rearrange("b i j -> b (i j)"))
         load_core(0,0)
         load_core(0,1)
         load_core(1,0)
-        nc.sync.dma_start(out=t_sb[0][:], in_=t2.rearrange("b p q -> b (p q)"))
         load_core(1,1)
-        nc.sync.dma_start(out=t_sb[1][:], in_=t3.rearrange("b p q -> b (p q)"))
         load_core(2,0)
-        nc.sync.dma_start(out=x_sb[:], in_=x.rearrange("b i j -> b (i j)"))
         load_core(3,0)
-        nc.sync.dma_start(out=km1_sb[:], in_=km1.rearrange("i j n -> (i j) n"))
-        nc.sync.dma_start(out=b1_rows[0:1, :], in_=b1.unsqueeze(0))
         load_core(2,1)
         load_core(3,1)
+        nc.sync.dma_start(out=km1_sb[:], in_=km1.rearrange("i j n -> (i j) n"))
+        nc.sync.dma_start(out=b1_rows[0:1, :], in_=b1.unsqueeze(0))
         load_core(3,2)
         gain_bias_bf16 = keep.tile([P, 2, N_BANKS * PACK], BF16)
         with nc.allow_non_contiguous_dma(reason="two vectors of 2048, in pieces of 8 bytes"):
@@ -161,15 +162,16 @@ def tile_pinmodel_pa_kernel(
                 stop=(c == PASSES - 1),
             )
 
-        def keep_warm(passes):
-            c, g = 3, 3
+        spare = [spare_pool.tile([P, BANK], F32, name="spare_ps", tag="spare")]
+
+        def keep_warm(passes, c=3, g=3, own=False):
             cols = slice(g * BANK, (g + 1) * BANK)
-            spare = work.tile([P, BANK], F32, name="spare", tag="work")
+            lhs = slice(g * BANK, g * BANK + P)
             for repeat in range(passes):
                 nc.tensor.matmul_mx(
-                    out=spare[:],
-                    lhsT=t_codes[:, c, :].bitcast(FP8X4),
-                    lhsT_scale=t_scales[:, c, :],
+                    out=spare[0][:],
+                    lhsT=c_codes[:, c, lhs].bitcast(FP8X4) if own else t_codes[:, c, :].bitcast(FP8X4),
+                    lhsT_scale=c_scales[:, c, lhs] if own else t_scales[:, c, :],
                     rhs=c_codes[:, c, cols].bitcast(FP8X4),
                     rhs_scale=c_scales[:, c, cols],
                     start=True,
@@ -252,70 +254,80 @@ def tile_pinmodel_pa_kernel(
                 accum_out=stats[:, g, 2:3],
             )
 
+        transpose_t(0)
+        transpose_t(1)
+        transpose_x()
+        keep_t(0)
+        keep_t(1)
+        keep_x()
+        quantize_t(0)
+        quantize_t(1)
         regroup_bank(0, 0)
         regroup_bank(0, 1)
         quantize_bank(0, 0)
+        multiply_bank(0, 0)
+        keep_warm(1, 0, 0)
         regroup_bank(0, 2)
         quantize_bank(0, 1)
+        multiply_bank(0, 1)
+        keep_warm(1, 0, 1)
         regroup_bank(0, 3)
         quantize_bank(0, 2)
+        multiply_bank(0, 2)
+        keep_warm(1, 0, 2)
         regroup_bank(1, 0)
         quantize_bank(0, 3)
-        transpose_t(0)
+        multiply_bank(0, 3)
+        keep_warm(1, 0, 3)
         regroup_bank(1, 1)
         quantize_bank(1, 0)
-        keep_t(0)
+        multiply_bank(1, 0)
+        keep_warm(1, 1, 0)
         regroup_bank(1, 2)
         quantize_bank(1, 1)
-        quantize_t(0)
-        transpose_t(1)
-        regroup_bank(1, 3)
-        multiply_bank(0, 0)
-        multiply_bank(0, 1)
-        multiply_bank(0, 2)
-        multiply_bank(0, 3)
-        multiply_bank(1, 0)
         multiply_bank(1, 1)
-        keep_t(1)
+        keep_warm(1, 1, 1)
+        regroup_bank(1, 3)
         quantize_bank(1, 2)
         multiply_bank(1, 2)
-        quantize_t(1)
+        keep_warm(1, 1, 2)
         regroup_bank(2, 0)
         quantize_bank(1, 3)
         multiply_bank(1, 3)
-        transpose_x()
+        keep_warm(1, 1, 3)
         regroup_bank(2, 1)
-        keep_x()
         quantize_bank(2, 0)
         multiply_bank(2, 0)
+        keep_warm(1, 2, 0)
         regroup_bank(3, 0)
         quantize_bank(2, 1)
         multiply_bank(2, 1)
-        order_1(0)
-        order_1(1)
         regroup_bank(3, 1)
         quantize_bank(3, 0)
         multiply_bank(3, 0)
-        keep_order_1(0)
-        keep_order_1(1)
-        order_1(2)
-        order_1(3)
+        keep_warm(1, 3, 0)
         quantize_bank(3, 1)
         multiply_bank(3, 1)
-        add_orders(0)
         regroup_bank(2, 2)
         regroup_bank(2, 3)
+        order_1(0)
+        order_1(1)
         quantize_bank(2, 2)
         multiply_bank(2, 2)
         regroup_bank(3, 2)
         quantize_bank(2, 3)
         multiply_bank(2, 3)
-        regroup_bank(3, 3)
-        keep_order_1(2)
-        keep_order_1(3)
+        keep_order_1(0)
         quantize_bank(3, 2)
         multiply_bank(3, 2)
+        keep_order_1(1)
+        order_1(2)
+        order_1(3)
+        add_orders(0)
+        regroup_bank(3, 3)
         add_orders(1)
+        keep_order_1(2)
+        keep_order_1(3)
         quantize_bank(3, 3)
         multiply_bank(3, 3)
         keep_warm(8)
@@ -346,7 +358,7 @@ def tile_pinmodel_pa_kernel(
         y_grouped = keep.tile([P, N_BANKS, P, PACK], BF16, align_bytes=64)
         y_codes = keep.tile([P, N_BANKS, P], U32, align_bytes=64)
         y_scales = keep.tile([P, N_BANKS, P], U8, align_bytes=64)
-        z_banks = [(work, "work")] * 4 + [(acc_pool, "acc%d" % g) for g in range(1, N_BANKS)] + [(work, "work")]
+        z_banks = [(work, "work")] * 3 + [(spare_pool, "spare")] + [(acc_pool, "acc%d" % g) for g in range(1, N_BANKS)] + [(work, "work")]
         zT = {}
 
         def normalise(g, first=0, last=PACK):
@@ -433,6 +445,7 @@ def tile_pinmodel_pa_kernel(
         apply_gain(3, 0, False)
         apply_gain(3, 1, False)
         apply_gain(0, 1, True)
+        spare[0] = work.tile([P, BANK], F32, name="spare2", tag="work")
         keep_warm(3)
         out_ps = [
             acc_pool.tile([P, OUT // 2], F32, name="out_ps0", tag="acc0"),

@@ -294,7 +294,7 @@ def tile_pinmodel_pa_kernel(
         regroup_bank(2, 0)
         quantize_bank(1, 3)
         multiply_bank(1, 3)
-        keep_warm(1, 1, 3)
+        keep_warm(2, 1, 3)
         regroup_bank(2, 1)
         quantize_bank(2, 0)
         multiply_bank(2, 0)
@@ -302,10 +302,11 @@ def tile_pinmodel_pa_kernel(
         regroup_bank(3, 0)
         quantize_bank(2, 1)
         multiply_bank(2, 1)
+        keep_warm(1, 2, 1)
         regroup_bank(3, 1)
         quantize_bank(3, 0)
         multiply_bank(3, 0)
-        keep_warm(1, 3, 0)
+        keep_warm(2, 3, 0)
         quantize_bank(3, 1)
         multiply_bank(3, 1)
         regroup_bank(2, 2)
@@ -320,6 +321,7 @@ def tile_pinmodel_pa_kernel(
         keep_order_1(0)
         quantize_bank(3, 2)
         multiply_bank(3, 2)
+        keep_warm(1, 3, 2)
         keep_order_1(1)
         order_1(2)
         order_1(3)
@@ -330,7 +332,7 @@ def tile_pinmodel_pa_kernel(
         keep_order_1(3)
         quantize_bank(3, 3)
         multiply_bank(3, 3)
-        keep_warm(8)
+        keep_warm(10)
         bank_mean(0)
         bank_squares(0)
         bank_mean(1)

@@ -128,7 +128,7 @@ def tile_pinmodel_pa_kernel(
         acc = [acc_pool.tile([P, BANK], F32, name="acc%d" % g) for g in range(N_BANKS)]
         o1 = keep.tile([P, N_BANKS, PACK, P], F32)
         o = keep.tile([P, N_BANKS, PACK, P], F32)
-        stats = keep.tile([P, N_BANKS + 1, 3], F32)
+        stats = keep.tile([P, N_BANKS + 3, 3], F32)
         nc.vector.memset(stats[:], float(BANK))
         sums = keep.tile([P, N_BANKS], F32)
         squares = keep.tile([P, N_BANKS, BANK], BF16)
@@ -164,12 +164,12 @@ def tile_pinmodel_pa_kernel(
 
         spare = [spare_pool.tile([P, BANK], F32, name="spare_ps", tag="spare")]
 
-        def keep_warm(passes, c=3, g=3, own=False):
+        def keep_warm(passes, c=3, g=3, own=False, bank=None):
             cols = slice(g * BANK, (g + 1) * BANK)
             lhs = slice(g * BANK, g * BANK + P)
             for repeat in range(passes):
                 nc.tensor.matmul_mx(
-                    out=spare[0][:],
+                    out=bank[:] if bank is not None else spare[0][:],
                     lhsT=c_codes[:, c, lhs].bitcast(FP8X4) if own else t_codes[:, c, :].bitcast(FP8X4),
                     lhsT_scale=c_scales[:, c, lhs] if own else t_scales[:, c, :],
                     rhs=c_codes[:, c, cols].bitcast(FP8X4),
@@ -237,6 +237,17 @@ def tile_pinmodel_pa_kernel(
                 op0=ALU.mult,
                 op1=ALU.add,
                 accum_out=sums[:, g : g + 1] if g < N_BANKS - 1 else None,
+            )
+
+        def add_last_bank(half):
+            t = slice(2 * half, 2 * half + 2)
+            nc.vector.scalar_tensor_tensor(
+                out=o[:, N_BANKS - 1, t, :],
+                in0=acc[N_BANKS - 1][:].rearrange("r (p t) -> r t p", t=PACK)[:, t, :],
+                scalar=1.0,
+                in1=o1[:, N_BANKS - 1, t, :],
+                op0=ALU.mult,
+                op1=ALU.add,
             )
 
         def bank_mean(g):
@@ -332,7 +343,7 @@ def tile_pinmodel_pa_kernel(
         keep_order_1(3)
         quantize_bank(3, 3)
         multiply_bank(3, 3)
-        keep_warm(10)
+        keep_warm(2)
         bank_mean(0)
         bank_squares(0)
         bank_mean(1)
@@ -340,16 +351,24 @@ def tile_pinmodel_pa_kernel(
         add_orders(2)
         bank_mean(2)
         bank_squares(2)
-        add_orders(3)
-        nc.vector.bn_stats(
-            out=stats[:, N_BANKS - 1 :, :].rearrange("r g s -> r (g s)"),
-            in_=o[:, N_BANKS - 1, :, :].rearrange("r t p -> r (t p)"),
-        )
+        for half in range(2):
+            add_last_bank(half)
+        for half in range(2):
+            nc.vector.bn_stats(
+                out=stats[:, N_BANKS - 1 + 2 * half : N_BANKS + 1 + 2 * half, :].rearrange("r g s -> r (g s)"),
+                in_=o[:, N_BANKS - 1, 2 * half : 2 * half + 2, :].rearrange("r t p -> r (t p)"),
+            )
+
+        keep_warm(6, bank=acc[3])
 
         gain_bias = keep.tile([P, 2, N_BANKS * PACK], F32)
         nc.scalar.copy(out=gain_bias[:], in_=gain_bias_bf16[:])
         mean_var = keep.tile([P, 2], F32)
         nc.vector.bn_aggr(out=mean_var[:], in_=stats[:].rearrange("r g s -> r (g s)"))
+        minus_mean = keep.tile([P, 1], F32)
+        nc.vector.tensor_scalar(
+            out=minus_mean[:], in0=mean_var[:, 0:1], scalar1=-1.0, scalar2=None, op0=ALU.mult
+        )
         rstd = keep.tile([P, 1], F32)
         nc.scalar.activation(
             out=rstd[:], in_=mean_var[:, 1:2], func=ACT.Abs_reciprocal_sqrt, bias=eps[:], scale=1.0
@@ -371,6 +390,17 @@ def tile_pinmodel_pa_kernel(
                 scalar2=rstd[:],
                 op0=ALU.subtract,
                 op1=ALU.mult,
+            )
+
+        def normalise_on_scalar(g):
+            offset = keep.tile([P, 1], F32, name="offset")
+            nc.scalar.activation(out=offset[:], in_=minus_mean[:], func=ACT.Copy, scale=rstd[:])
+            nc.scalar.activation(
+                out=z[:, g, :, :].rearrange("r t p -> r (t p)"),
+                in_=o[:, g, :, :].rearrange("r t p -> r (t p)"),
+                func=ACT.Identity,
+                bias=offset[:],
+                scale=rstd[:],
             )
 
         def transpose_z(g, half):
@@ -436,17 +466,17 @@ def tile_pinmodel_pa_kernel(
         normalise(2)
         transpose_z(2, 0)
         transpose_z(2, 1)
-        normalise(3)
+        normalise_on_scalar(3)
         transpose_z(3, 0)
         apply_gain(0, 0, False)
         transpose_z(3, 1)
         apply_gain(1, 0, False)
-        apply_gain(1, 1, False)
         apply_gain(2, 0, False)
         apply_gain(2, 1, False)
         apply_gain(3, 0, False)
         apply_gain(3, 1, False)
         apply_gain(0, 1, True)
+        apply_gain(1, 1, True)
         spare[0] = work.tile([P, BANK], F32, name="spare2", tag="work")
         keep_warm(3)
         out_ps = [

@@ -31,6 +31,7 @@ FLOPS = 2 * P * (K1 + 2 * KR) * DIM + 2 * P * DIM * OUT
 
 PIECES = ((1024,1024),(1024,1024),(1024,1024),(1024,512,512))
 VECTOR_COLS = (256,256,256,256)
+LAST = (96, 320)
 
 
 def regroup(copy, grouped, rows):
@@ -135,11 +136,19 @@ def tile_pinmodel_pa_kernel(
         xT = keep.tile([P, P], BF16)
         grouped = {}
 
+        def gpsimd_copy(out, in_):
+            nc.gpsimd.tensor_scalar(out=out, in0=in_, scalar1=1.0, scalar2=0.0, op0=ALU.mult, op1=ALU.add)
+
         def regroup_bank(c, g):
             tile = grouped_pool.tile([P, BANK, PACK], BF16, name="grouped_bank", align_bytes=64)
-            split = VECTOR_COLS[c]
-            regroup(nc.vector.tensor_copy, tile[:, :split, :], raw[(c, g)][:, :, :split])
-            regroup(nc.scalar.copy, tile[:, split:, :], raw[(c, g)][:, :, split:])
+            split, end = VECTOR_COLS[4] if c >= 2 and g >= 2 and len(VECTOR_COLS) > 4 else VECTOR_COLS[c], BANK
+            if (c, g) == (3, 3):
+                if LAST != (256, 512): split, end = LAST
+            if split:
+                regroup(nc.vector.tensor_copy, tile[:, :split, :], raw[(c, g)][:, :, :split])
+            regroup(nc.scalar.copy, tile[:, split:end, :], raw[(c, g)][:, :, split:end])
+            if end < BANK:
+                regroup(gpsimd_copy, tile[:, end:, :], raw[(c, g)][:, :, end:])
             grouped[(c, g)] = tile
 
         def quantize_bank(c, g):
@@ -332,12 +341,11 @@ def tile_pinmodel_pa_kernel(
         keep_order_1(0)
         quantize_bank(3, 2)
         multiply_bank(3, 2)
-        keep_warm(1, 3, 2)
         keep_order_1(1)
+        regroup_bank(3, 3)
         order_1(2)
         order_1(3)
         add_orders(0)
-        regroup_bank(3, 3)
         add_orders(1)
         keep_order_1(2)
         keep_order_1(3)
@@ -351,14 +359,13 @@ def tile_pinmodel_pa_kernel(
         add_orders(2)
         bank_mean(2)
         bank_squares(2)
-        for half in range(2):
-            add_last_bank(half)
+        add_last_bank(0)
+        add_last_bank(1)
         for half in range(2):
             nc.vector.bn_stats(
                 out=stats[:, N_BANKS - 1 + 2 * half : N_BANKS + 1 + 2 * half, :].rearrange("r g s -> r (g s)"),
                 in_=o[:, N_BANKS - 1, 2 * half : 2 * half + 2, :].rearrange("r t p -> r (t p)"),
             )
-
         keep_warm(6, bank=acc[3])
 
         gain_bias = keep.tile([P, 2, N_BANKS * PACK], F32)

from contextlib import ExitStack

import concourse.mybir as mybir
from concourse.masks import make_identity

F32 = mybir.dt.float32
BF16 = mybir.dt.bfloat16
U32 = mybir.dt.uint32
U8 = mybir.dt.uint8
I32 = mybir.dt.int32
FP8X4 = mybir.dt.float8_e4m3fn_x4
ALU = mybir.AluOpType
ACT = mybir.ActivationFunctionType

P = 128
PACK = 4
K_PASS = P * PACK
K1 = 128
KR = 1024
DIM = 2048
OUT = 512
BANK = 512
N_BANKS = DIM // BANK
CORE_PASSES = KR // K_PASS
PASSES = 2 * CORE_PASSES
RUN = 4
EPS = 1e-5

FLOPS = 2 * P * (K1 + 2 * KR) * DIM + 2 * P * DIM * OUT


PIECES = ((1024,1024),(1024,1024),(1024,1024),(1024,512,512))
VECTOR_COLS = (256,256,256,256)
LAST = (96, 320)


def regroup(copy, grouped, rows):
    copy(
        out=grouped.rearrange("p (c i) j -> p c j i", i=RUN),
        in_=rows.rearrange("p j (c i) -> p c j i", i=RUN),
    )


def tile_pinmodel_pa_kernel(
    tc, x, km1, b1, t2, core2, t3, core3, ln_g, ln_b, fc_w_words, fc_w_scales, fc_b, out
):
    nc = tc.nc
    with ExitStack() as ctx:
        keep = ctx.enter_context(tc.tile_pool(name="keep", bufs=1))
        grouped_pool = ctx.enter_context(tc.tile_pool(name="grouped", bufs=4))
        acc_pool = ctx.enter_context(tc.psum_pool(name="acc", bufs=1))
        work = ctx.enter_context(tc.psum_pool(name="work", bufs=3))
        spare_pool = ctx.enter_context(tc.psum_pool(name="spare", bufs=1))
        ctx.enter_context(tc.manual_schedule())

        b1_rows = keep.tile([P, DIM], BF16)
        nc.gpsimd.memset(b1_rows[:].bitcast(I32), 0)
        ident_bf16 = keep.tile([P, P], BF16)
        make_identity(nc, ident_bf16[:])
        ident_f32 = keep.tile([P, P], F32)
        make_identity(nc, ident_f32[:])
        ones = keep.tile([P, P], BF16)
        nc.vector.memset(ones[:], 1.0)
        eps = keep.tile([P, 1], F32)
        nc.vector.memset(eps[:], EPS)
        w_planes = keep.tile([P, OUT], U8, align_bytes=64)
        nc.vector.memset(w_planes[:].bitcast(I32), 0)
        warm = keep.tile([P, 1], F32)
        nc.scalar.activation(out=warm[:], in_=eps[:], func=ACT.Abs_reciprocal_sqrt)

        cores = [t.rearrange("p q n -> (p q) n") for t in (core2, core3)]
        raw = {}

        def load_core(c, piece):
            width = PIECES[c][piece]
            begin = sum(PIECES[c][:piece])
            first = (c % CORE_PASSES) * K_PASS
            rows = cores[c // CORE_PASSES][first : first + K_PASS, :]
            raw_tile = keep.tile([P, PACK, width], BF16, name="raw%d_%d" % (c, piece))
            nc.sync.dma_start(
                out=raw_tile[:],
                in_=rows.rearrange("(p j) n -> p j n", j=PACK)[:, :, begin : begin + width],
            )
            for b in range(width // BANK):
                raw[(c, begin // BANK + b)] = raw_tile[:, :, b * BANK : (b + 1) * BANK]

        x_sb = keep.tile([P, K1], BF16)
        t_sb = [keep.tile([P, KR], BF16, name="t_sb%d" % i) for i in range(2)]
        km1_sb = keep.tile([P, DIM], BF16)
        nc.sync.dma_start(out=t_sb[0][:], in_=t2.rearrange("b p q -> b (p q)"))
        nc.sync.dma_start(out=t_sb[1][:], in_=t3.rearrange("b p q -> b (p q)"))
        nc.sync.dma_start(out=x_sb[:], in_=x.rearrange("b i j -> b (i j)"))
        load_core(0,0)
        load_core(0,1)
        load_core(1,0)
        load_core(1,1)
        load_core(2,0)
        load_core(3,0)
        load_core(2,1)
        load_core(3,1)
        nc.sync.dma_start(out=km1_sb[:], in_=km1.rearrange("i j n -> (i j) n"))
        nc.sync.dma_start(out=b1_rows[0:1, :], in_=b1.unsqueeze(0))
        load_core(3,2)
        gain_bias_bf16 = keep.tile([P, 2, N_BANKS * PACK], BF16)
        with nc.allow_non_contiguous_dma(reason="two vectors of 2048, in pieces of 8 bytes"):
            for i, vec in enumerate((ln_g, ln_b)):
                nc.sync.dma_start(
                    out=gain_bias_bf16[:, i, :].rearrange("p (g t) -> p g t", t=PACK),
                    in_=vec.rearrange("(g p t) -> p g t", p=P, t=PACK),
                )
        scale_words = fc_w_scales.bitcast(I32)
        for quadrant in range(4):
            nc.sync.dma_start(
                out=w_planes[:].bitcast(I32)[32 * quadrant : 32 * quadrant + 16, :],
                in_=scale_words[:, 4 * quadrant : 4 * quadrant + 4, :],
            )
        w_words = keep.tile([P, N_BANKS, OUT], U32, align_bytes=64)
        nc.sync.dma_start(
            out=w_words[:].bitcast(I32),
            in_=fc_w_words.rearrange("g p n t -> p g (n t)").bitcast(I32),
        )
        fc_b_all = keep.tile([P, OUT], BF16)
        nc.sync.dma_start(out=fc_b_all[:], in_=fc_b.partition_broadcast(P))

        c_codes = keep.tile([P, PASSES, DIM], U32, align_bytes=64)
        c_scales = keep.tile([P, PASSES, DIM], U8, align_bytes=64)
        t_codes = keep.tile([P, PASSES, P], U32, align_bytes=64)
        t_scales = keep.tile([P, PASSES, P], U8, align_bytes=64)
        acc = [acc_pool.tile([P, BANK], F32, name="acc%d" % g) for g in range(N_BANKS)]
        o1 = keep.tile([P, N_BANKS, PACK, P], F32)
        o = keep.tile([P, N_BANKS, PACK, P], F32)
        stats = keep.tile([P, N_BANKS + 3, 3], F32)
        nc.vector.memset(stats[:], float(BANK))
        sums = keep.tile([P, N_BANKS], F32)
        squares = keep.tile([P, N_BANKS, BANK], BF16)
        xT = keep.tile([P, P], BF16)
        grouped = {}

        def gpsimd_copy(out, in_):
            nc.gpsimd.tensor_scalar(out=out, in0=in_, scalar1=1.0, scalar2=0.0, op0=ALU.mult, op1=ALU.add)

        def regroup_bank(c, g):
            tile = grouped_pool.tile([P, BANK, PACK], BF16, name="grouped_bank", align_bytes=64)
            split, end = VECTOR_COLS[4] if c >= 2 and g >= 2 and len(VECTOR_COLS) > 4 else VECTOR_COLS[c], BANK
            if (c, g) == (3, 3):
                if LAST != (256, 512): split, end = LAST
            if split:
                regroup(nc.vector.tensor_copy, tile[:, :split, :], raw[(c, g)][:, :, :split])
            regroup(nc.scalar.copy, tile[:, split:end, :], raw[(c, g)][:, :, split:end])
            if end < BANK:
                regroup(gpsimd_copy, tile[:, end:, :], raw[(c, g)][:, :, end:])
            grouped[(c, g)] = tile

        def quantize_bank(c, g):
            cols = slice(g * BANK, (g + 1) * BANK)
            nc.vector.quantize_mx(
                out=c_codes[:, c, cols].bitcast(FP8X4),
                scales=c_scales[:, c, cols],
                in_=grouped[(c, g)][:].rearrange("p w j -> p (w j)"),
            )

        def multiply_bank(c, g):
            cols = slice(g * BANK, (g + 1) * BANK)
            nc.tensor.matmul_mx(
                out=acc[g][:],
                lhsT=t_codes[:, c, :].bitcast(FP8X4),
                lhsT_scale=t_scales[:, c, :],
                rhs=c_codes[:, c, cols].bitcast(FP8X4),
                rhs_scale=c_scales[:, c, cols],
                start=(c == 0),
                stop=(c == PASSES - 1),
            )

        spare = [spare_pool.tile([P, BANK], F32, name="spare_ps", tag="spare")]

        def keep_warm(passes, c=3, g=3, own=False, bank=None):
            cols = slice(g * BANK, (g + 1) * BANK)
            lhs = slice(g * BANK, g * BANK + P)
            for repeat in range(passes):
                nc.tensor.matmul_mx(
                    out=bank[:] if bank is not None else spare[0][:],
                    lhsT=c_codes[:, c, lhs].bitcast(FP8X4) if own else t_codes[:, c, :].bitcast(FP8X4),
                    lhsT_scale=c_scales[:, c, lhs] if own else t_scales[:, c, :],
                    rhs=c_codes[:, c, cols].bitcast(FP8X4),
                    rhs_scale=c_scales[:, c, cols],
                    start=True,
                    stop=True,
                )

        in_psum = {}

        def transpose_x():
            xT_ps = work.tile([P, P], BF16, tag="work")
            nc.tensor.transpose(out=xT_ps[:], in_=x_sb[:], identity=ident_bf16[:])
            in_psum["x"] = xT_ps

        def keep_x():
            nc.scalar.copy(out=xT[:], in_=in_psum["x"][:])

        t_grouped = {}

        def transpose_t(i):
            words = t_sb[i][:].bitcast(F32)
            tT_ps = work.tile([P, CORE_PASSES, 2, P], F32, tag="work")
            for g in range(CORE_PASSES):
                for u in range(2):
                    nc.tensor.transpose(
                        out=tT_ps[:, g, u, :],
                        in_=words[:, g * K_PASS // 2 + u : (g + 1) * K_PASS // 2 : 2],
                        identity=ident_f32[:],
                    )
            in_psum[i] = tT_ps

        def keep_t(i):
            t_grouped[i] = keep.tile([P, KR], BF16, name="t_grouped%d" % i, align_bytes=64)
            nc.scalar.copy(
                out=t_grouped[i][:].bitcast(F32).rearrange("p (g r u) -> p g r u", g=CORE_PASSES, u=2),
                in_=in_psum[i][:].rearrange("p g u r -> p g r u"),
            )

        def quantize_t(i):
            passes = slice(i * CORE_PASSES, (i + 1) * CORE_PASSES)
            nc.vector.quantize_mx(
                out=t_codes[:, passes, :].rearrange("p g r -> p (g r)").bitcast(FP8X4),
                scales=t_scales[:, passes, :].rearrange("p g r -> p (g r)"),
                in_=t_grouped[i][:],
            )

        o1_ps = {}

        def order_1(g):
            cols = slice(g * BANK, (g + 1) * BANK)
            o1_ps[g] = work.tile([P, BANK], F32, name="o1_ps", tag="work")
            nc.tensor.matmul(out=o1_ps[g][:], lhsT=xT[:], rhs=km1_sb[:, cols], start=True, stop=False)
            nc.tensor.matmul(out=o1_ps[g][:], lhsT=ones[:], rhs=b1_rows[:, cols], start=False, stop=True)

        def keep_order_1(g):
            nc.scalar.copy(out=o1[:, g, :, :], in_=o1_ps[g][:].rearrange("r (p t) -> r t p", t=PACK))

        def add_orders(g):
            nc.vector.scalar_tensor_tensor(
                out=o[:, g, :, :],
                in0=acc[g][:].rearrange("r (p t) -> r t p", t=PACK),
                scalar=1.0,
                in1=o1[:, g, :, :],
                op0=ALU.mult,
                op1=ALU.add,
                accum_out=sums[:, g : g + 1] if g < N_BANKS - 1 else None,
            )

        def add_last_bank(half):
            t = slice(2 * half, 2 * half + 2)
            nc.vector.scalar_tensor_tensor(
                out=o[:, N_BANKS - 1, t, :],
                in0=acc[N_BANKS - 1][:].rearrange("r (p t) -> r t p", t=PACK)[:, t, :],
                scalar=1.0,
                in1=o1[:, N_BANKS - 1, t, :],
                op0=ALU.mult,
                op1=ALU.add,
            )

        def bank_mean(g):
            nc.gpsimd.tensor_scalar(
                out=stats[:, g, 1:2], in0=sums[:, g : g + 1], scalar1=1.0 / BANK, scalar2=None, op0=ALU.mult
            )

        def bank_squares(g):
            nc.scalar.activation(
                out=squares[:, g, :],
                in_=o[:, g, :, :].rearrange("r t p -> r (t p)"),
                func=ACT.Square,
                bias=stats[:, g, 1:2],
                scale=-1.0,
                accum_out=stats[:, g, 2:3],
            )

        transpose_t(0)
        transpose_t(1)
        transpose_x()
        keep_t(0)
        keep_t(1)
        keep_x()
        quantize_t(0)
        quantize_t(1)
        regroup_bank(0, 0)
        regroup_bank(0, 1)
        quantize_bank(0, 0)
        multiply_bank(0, 0)
        keep_warm(1, 0, 0)
        regroup_bank(0, 2)
        quantize_bank(0, 1)
        multiply_bank(0, 1)
        keep_warm(1, 0, 1)
        regroup_bank(0, 3)
        quantize_bank(0, 2)
        multiply_bank(0, 2)
        keep_warm(1, 0, 2)
        regroup_bank(1, 0)
        quantize_bank(0, 3)
        multiply_bank(0, 3)
        keep_warm(1, 0, 3)
        regroup_bank(1, 1)
        quantize_bank(1, 0)
        multiply_bank(1, 0)
        keep_warm(1, 1, 0)
        regroup_bank(1, 2)
        quantize_bank(1, 1)
        multiply_bank(1, 1)
        keep_warm(1, 1, 1)
        regroup_bank(1, 3)
        quantize_bank(1, 2)
        multiply_bank(1, 2)
        keep_warm(1, 1, 2)
        regroup_bank(2, 0)
        quantize_bank(1, 3)
        multiply_bank(1, 3)
        keep_warm(2, 1, 3)
        regroup_bank(2, 1)
        quantize_bank(2, 0)
        multiply_bank(2, 0)
        keep_warm(1, 2, 0)
        regroup_bank(3, 0)
        quantize_bank(2, 1)
        multiply_bank(2, 1)
        keep_warm(1, 2, 1)
        regroup_bank(3, 1)
        quantize_bank(3, 0)
        multiply_bank(3, 0)
        keep_warm(2, 3, 0)
        quantize_bank(3, 1)
        multiply_bank(3, 1)
        regroup_bank(2, 2)
        regroup_bank(2, 3)
        order_1(0)
        order_1(1)
        quantize_bank(2, 2)
        multiply_bank(2, 2)
        regroup_bank(3, 2)
        quantize_bank(2, 3)
        multiply_bank(2, 3)
        keep_order_1(0)
        quantize_bank(3, 2)
        multiply_bank(3, 2)
        keep_order_1(1)
        regroup_bank(3, 3)
        order_1(2)
        order_1(3)
        add_orders(0)
        add_orders(1)
        keep_order_1(2)
        keep_order_1(3)
        quantize_bank(3, 3)
        multiply_bank(3, 3)
        keep_warm(2)
        bank_mean(0)
        bank_squares(0)
        bank_mean(1)
        bank_squares(1)
        add_orders(2)
        bank_mean(2)
        bank_squares(2)
        add_last_bank(0)
        add_last_bank(1)
        for half in range(2):
            nc.vector.bn_stats(
                out=stats[:, N_BANKS - 1 + 2 * half : N_BANKS + 1 + 2 * half, :].rearrange("r g s -> r (g s)"),
                in_=o[:, N_BANKS - 1, 2 * half : 2 * half + 2, :].rearrange("r t p -> r (t p)"),
            )
        keep_warm(6, bank=acc[3])

        gain_bias = keep.tile([P, 2, N_BANKS * PACK], F32)
        nc.scalar.copy(out=gain_bias[:], in_=gain_bias_bf16[:])
        mean_var = keep.tile([P, 2], F32)
        nc.vector.bn_aggr(out=mean_var[:], in_=stats[:].rearrange("r g s -> r (g s)"))
        minus_mean = keep.tile([P, 1], F32)
        nc.vector.tensor_scalar(
            out=minus_mean[:], in0=mean_var[:, 0:1], scalar1=-1.0, scalar2=None, op0=ALU.mult
        )
        rstd = keep.tile([P, 1], F32)
        nc.scalar.activation(
            out=rstd[:], in_=mean_var[:, 1:2], func=ACT.Abs_reciprocal_sqrt, bias=eps[:], scale=1.0
        )

        z = keep.tile([P, N_BANKS, PACK, P], F32)
        y_planes = keep.tile([P, N_BANKS, PACK, P], BF16)
        y_grouped = keep.tile([P, N_BANKS, P, PACK], BF16, align_bytes=64)
        y_codes = keep.tile([P, N_BANKS, P], U32, align_bytes=64)
        y_scales = keep.tile([P, N_BANKS, P], U8, align_bytes=64)
        z_banks = [(work, "work")] * 3 + [(spare_pool, "spare")] + [(acc_pool, "acc%d" % g) for g in range(1, N_BANKS)] + [(work, "work")]
        zT = {}

        def normalise(g, first=0, last=PACK):
            nc.vector.tensor_scalar(
                out=z[:, g, first:last, :],
                in0=o[:, g, first:last, :],
                scalar1=mean_var[:, 0:1],
                scalar2=rstd[:],
                op0=ALU.subtract,
                op1=ALU.mult,
            )

        def normalise_on_scalar(g):
            offset = keep.tile([P, 1], F32, name="offset")
            nc.scalar.activation(out=offset[:], in_=minus_mean[:], func=ACT.Copy, scale=rstd[:])
            nc.scalar.activation(
                out=z[:, g, :, :].rearrange("r t p -> r (t p)"),
                in_=o[:, g, :, :].rearrange("r t p -> r (t p)"),
                func=ACT.Identity,
                bias=offset[:],
                scale=rstd[:],
            )

        def transpose_z(g, half):
            pool, tag = z_banks[2 * g + half]
            zT[(g, half)] = pool.tile([P, 2, P], F32, name="zT_ps", tag=tag)
            for e in range(2):
                nc.tensor.transpose(
                    out=zT[(g, half)][:, e, :], in_=z[:, g, 2 * half + e, :], identity=ident_f32[:]
                )

        def apply_gain(g, half, on_vector):
            for e in range(2):
                t = 2 * half + e
                k = g * PACK + t
                gain = gain_bias[:, 0, k : k + 1]
                bias = gain_bias[:, 1, k : k + 1]
                if on_vector:
                    nc.vector.tensor_scalar(
                        out=y_planes[:, g, t, :],
                        in0=zT[(g, half)][:, e, :],
                        scalar1=gain,
                        scalar2=bias,
                        op0=ALU.mult,
                        op1=ALU.add,
                    )
                else:
                    nc.scalar.activation(
                        out=y_planes[:, g, t, :],
                        in_=zT[(g, half)][:, e, :],
                        func=ACT.Identity,
                        bias=bias,
                        scale=gain,
                    )

        def regroup_y(g):
            regroup(nc.vector.tensor_copy, y_grouped[:, g, :, :], y_planes[:, g, :, :])

        def multiply_y(g):
            nc.vector.quantize_mx(
                out=y_codes[:, g, :].bitcast(FP8X4),
                scales=y_scales[:, g, :],
                in_=y_grouped[:, g, :, :].rearrange("p r t -> p (r t)"),
            )
            for h in range(2):
                cols = slice(h * OUT // 2, (h + 1) * OUT // 2)
                nc.tensor.matmul_mx(
                    out=out_ps[h][:],
                    lhsT=y_codes[:, g, :].bitcast(FP8X4),
                    lhsT_scale=y_scales[:, g, :],
                    rhs=w_words[:, g, cols].bitcast(FP8X4),
                    rhs_scale=w_planes[PACK * g : P, cols],
                    start=(g == 0),
                    stop=(g == N_BANKS - 1),
                )

        normalise(0, 0, 2)
        transpose_z(0, 0)
        normalise(0, 2, 4)
        transpose_z(0, 1)
        normalise(1)
        transpose_z(1, 0)
        transpose_z(1, 1)
        normalise(2)
        transpose_z(2, 0)
        transpose_z(2, 1)
        normalise_on_scalar(3)
        transpose_z(3, 0)
        apply_gain(0, 0, False)
        transpose_z(3, 1)
        apply_gain(1, 0, False)
        apply_gain(2, 0, False)
        apply_gain(2, 1, False)
        apply_gain(3, 0, False)
        apply_gain(3, 1, False)
        apply_gain(0, 1, True)
        apply_gain(1, 1, True)
        spare[0] = work.tile([P, BANK], F32, name="spare2", tag="work")
        keep_warm(3)
        out_ps = [
            acc_pool.tile([P, OUT // 2], F32, name="out_ps0", tag="acc0"),
            work.tile([P, OUT // 2], F32, name="out_ps1", tag="work"),
        ]
        regroup_y(0)
        regroup_y(1)
        multiply_y(0)
        regroup_y(2)
        multiply_y(1)
        regroup_y(3)
        multiply_y(2)
        multiply_y(3)
        out_sb = keep.tile([P, OUT], F32)
        for h in range(2):
            cols = slice(h * OUT // 2, (h + 1) * OUT // 2)
            nc.vector.tensor_tensor(out=out_sb[:, cols], in0=out_ps[h][:], in1=fc_b_all[:, cols], op=ALU.add)
            nc.sync.dma_start(out=out.rearrange("b o n -> b (o n)")[:, cols], in_=out_sb[:, cols])
